import numpy as np
import ml_dtypes


def mxq(x, axis, fmt="e4m3"):
    dtype, down = {"e4m3": (ml_dtypes.float8_e4m3fn, 7), "e5m2": (ml_dtypes.float8_e5m2, 14)}[fmt]
    v = np.moveaxis(np.asarray(x, np.float32).astype(ml_dtypes.bfloat16).astype(np.float64), axis, -1)
    blocks = v.reshape(v.shape[:-1] + (-1, 32))
    amax = np.abs(blocks).max(-1, keepdims=True)
    byte = np.maximum(np.where(amax > 0, np.frexp(amax)[1] - 1 + 127, 0) - down, 1)
    scale = np.exp2(byte - 127.0)
    codes = (blocks / scale).astype(np.float32).astype(dtype).astype(np.float64)
    return np.moveaxis((codes * scale).reshape(v.shape), -1, axis)


WIDE = False


def mx_kscale(k):
    if not WIDE:
        return np.ones(k)
    levels = np.array([20, -20, 10, -10, 0])
    a = np.random.permutation(np.resize(levels, k // 512 * 4)).reshape(k // 512, 4)
    idx = np.arange(k)
    return np.exp2(a[idx // 512, idx % 128 // 32])


BF16 = ml_dtypes.bfloat16


def bf(x):
    return np.asarray(x, np.float32).astype(BF16)


def f64(x):
    return np.asarray(x).astype(np.float64)


B, D, C = 2048, 1024, 1024
SCALE = 100.0
GAMMA = 20.0
EPS = 1e-12
PULL = 2.0
KSCALE = 4.0
GSCALE = 16384.0


def l2_normalize(v, axis):
    sq = np.sum(v * v, axis=axis, keepdims=True)
    return v * (1.0 / np.sqrt(np.maximum(sq, EPS)))


def rbf_and_probs(x, kernel):
    e = l2_normalize(x, 1)
    w = l2_normalize(kernel, 0)
    dots = e @ w
    r = np.exp(-(2.0 - 2.0 * dots) / GAMMA)
    logits = SCALE * r
    z = np.exp(logits - logits.max(-1, keepdims=True))
    return r, z / z.sum(-1, keepdims=True)


def setup_inputs():
    u = mx_kscale(C)[None, :]
    gm = np.random.standard_normal((D, C))
    lab = np.random.randint(0, C, B)
    x = bf(PULL * gm[:, lab].T + np.random.standard_normal((B, D)))
    kernel0 = bf(gm * (KSCALE / np.sqrt(D)))
    g = bf(np.random.standard_normal((B, C)) * np.exp2(np.random.randint(-12, 1, (B, 1))) * GSCALE)
    r, p = rbf_and_probs(f64(x), f64(kernel0))
    return {"x": x, "kernel": bf(f64(kernel0) / u), "rbf": np.asarray(r, np.float32),
            "probs": np.asarray(p, np.float32), "grad_out": g}


def reference(x, kernel, rbf, probs, grad_out):
    xf = f64(x)
    kf = f64(kernel)
    p = f64(probs)
    g = f64(grad_out)
    rx = 1.0 / np.sqrt(np.maximum(np.sum(xf * xf, axis=1, keepdims=True), EPS))
    rk = 1.0 / np.sqrt(np.maximum(np.sum(kf * kf, axis=0, keepdims=True), EPS))
    dl = p * (g - np.sum(g * p, axis=1, keepdims=True))
    dk = dl * (SCALE * 2.0 / GAMMA) * f64(rbf) * rk
    de = mxq(dk, 1, "e5m2") @ mxq(kf, 1, "e4m3").T
    e = xf * rx
    return rx * (de - e * np.sum(de * e, axis=1, keepdims=True))

@@ -1,0 +1,270 @@
+from contextlib import ExitStack
+
+import concourse.mybir as mybir
+from concourse.masks import make_identity
+
+F32 = mybir.dt.float32
+BF16 = mybir.dt.bfloat16
+U32 = mybir.dt.uint32
+U8 = mybir.dt.uint8
+E4M3X4 = mybir.dt.float8_e4m3fn_x4
+E5M2X4 = mybir.dt.float8_e5m2_x4
+ACT = mybir.ActivationFunctionType
+ALU = mybir.AluOpType
+
+TOKENS, FEATURES, CLASSES = 2048, 1024, 1024
+P = 128
+PACK = 4
+K_PASS = P * PACK
+PASSES = CLASSES // K_PASS
+N_COLS = 512
+N_HALVES = FEATURES // N_COLS
+PAIR = 2
+PAIRS = TOKENS // (PAIR * P)
+D_TILES = FEATURES // P
+EPS = 1e-12
+LOGIT_SLOPE = 100.0 * 2.0 / 20.0
+
+FLOPS = 2 * TOKENS * FEATURES * CLASSES
+
+
+def tile_rbf_softmax_layer_t_v_kernel(tc, x, kernel, rbf, probs, grad_out, out):
+    nc = tc.nc
+
+    def by_pairs(dram):
+        return dram.rearrange("(q p j) c -> q p j c", p=P, j=PAIR)
+
+    x_pairs, rbf_pairs, probs_pairs, grad_pairs, out_pairs = (
+        by_pairs(x),
+        by_pairs(rbf),
+        by_pairs(probs),
+        by_pairs(grad_out),
+        by_pairs(out),
+    )
+
+    with ExitStack() as pools:
+        keep = pools.enter_context(tc.tile_pool(name="keep", bufs=1))
+        loads = pools.enter_context(tc.tile_pool(name="loads", bufs=3))
+        work = pools.enter_context(tc.tile_pool(name="work", bufs=3))
+        small = pools.enter_context(tc.tile_pool(name="small", bufs=4))
+        psum_dl = pools.enter_context(tc.psum_pool(name="psum_dl", bufs=2))
+        psum_rbf = pools.enter_context(tc.psum_pool(name="psum_rbf", bufs=2))
+        psum_de = pools.enter_context(tc.psum_pool(name="psum_de", bufs=4))
+
+        ident_f32 = keep.tile([P, P], F32)
+        make_identity(nc, ident_f32[:])
+        ident_bf16 = keep.tile([P, P], BF16)
+        make_identity(nc, ident_bf16[:])
+        one = keep.tile([P, 1], F32)
+        nc.vector.memset(one[:], 1.0)
+        warm = keep.tile([P, 1], F32)
+        nc.scalar.activation(out=warm[:], in_=one[:], func=ACT.Sqrt)
+
+        k_rows = keep.tile([P, D_TILES, CLASSES], BF16)
+        for i in range(0, D_TILES, 2):
+            nc.sync.dma_start(
+                out=k_rows[:, i : i + 2, :],
+                in_=kernel[i * P : (i + 2) * P, :].rearrange("(i p) c -> p i c", p=P),
+            )
+        k_grouped = keep.tile([P, PASSES, FEATURES, PACK], BF16, align_bytes=64)
+        for i in range(D_TILES):
+            k_turned = psum_de.tile([P, PASSES, PACK, P], BF16, tag="de")
+            for g in range(PASSES):
+                for t in range(PACK):
+                    c0 = g * K_PASS + t * P
+                    nc.tensor.transpose(k_turned[:, g, t, :], k_rows[:, i, c0 : c0 + P], ident_bf16[:])
+            grouped_view = k_grouped[:, :, i * P : (i + 1) * P, :]
+            turned_view = k_turned[:].rearrange("p g t r -> p g r t")
+            if i % 2 == 0:
+                nc.vector.tensor_copy(out=grouped_view, in_=turned_view)
+            else:
+                nc.scalar.copy(out=grouped_view, in_=turned_view)
+
+        k_codes = keep.tile([P, PASSES, FEATURES], U32, align_bytes=64)
+        k_scales = keep.tile([P, PASSES, FEATURES], U8, align_bytes=64)
+        for g in range(PASSES):
+            nc.vector.quantize_mx(
+                out=k_codes[:, g, :].bitcast(E4M3X4),
+                scales=k_scales[:, g, :],
+                in_=k_grouped[:, g, :, :].rearrange("p d t -> p (d t)"),
+            )
+
+        k_sumsq = [keep.tile([P, PACK], F32, name="k_sumsq%d" % g) for g in range(PASSES)]
+        for t in range(PACK):
+            squares_s = work.tile([P, FEATURES], BF16, tag="unread_s")
+            nc.scalar.activation(
+                out=squares_s[:], in_=k_grouped[:, 0, :, t], func=ACT.Square, accum_out=k_sumsq[0][:, t : t + 1]
+            )
+            squares_v = work.tile([P, FEATURES], BF16, tag="unread_v")
+            nc.vector.scalar_tensor_tensor(
+                out=squares_v[:],
+                in0=k_grouped[:, 1, :, t],
+                scalar=1.0,
+                in1=k_grouped[:, 1, :, t],
+                op0=ALU.mult,
+                op1=ALU.mult,
+                accum_out=k_sumsq[1][:, t : t + 1],
+            )
+        rk10 = []
+        for g in range(PASSES):
+            a = keep.tile([P, PACK], F32, name="k_a%d" % g)
+            nc.vector.tensor_scalar_max(out=a[:], in0=k_sumsq[g][:], scalar1=EPS)
+            inv_a = keep.tile([P, PACK], F32, name="k_inv_a%d" % g)
+            nc.vector.reciprocal(out=inv_a[:], in_=a[:])
+            y = keep.tile([P, PACK], F32, name="k_y%d" % g)
+            nc.scalar.activation(out=y[:], in_=inv_a[:], func=ACT.Sqrt)
+            yy = keep.tile([P, PACK], F32, name="k_yy%d" % g)
+            nc.vector.tensor_tensor(out=yy[:], in0=y[:], in1=y[:], op=ALU.mult)
+            ayy = keep.tile([P, PACK], F32, name="k_ayy%d" % g)
+            nc.vector.tensor_tensor(out=ayy[:], in0=yy[:], in1=a[:], op=ALU.mult)
+            step = keep.tile([P, PACK], F32, name="k_step%d" % g)
+            nc.vector.tensor_scalar(
+                out=step[:],
+                in0=ayy[:],
+                scalar1=-0.5 * LOGIT_SLOPE,
+                scalar2=1.5 * LOGIT_SLOPE,
+                op0=ALU.mult,
+                op1=ALU.add,
+            )
+            rk10_g = keep.tile([P, PACK], F32, name="rk10_%d" % g)
+            nc.vector.tensor_tensor(out=rk10_g[:], in0=y[:], in1=step[:], op=ALU.mult)
+            rk10.append(rk10_g)
+
+        for q in range(PAIRS):
+            probs_sb = loads.tile([P, PAIR, CLASSES], F32, tag="probs")
+            nc.sync.dma_start(out=probs_sb[:], in_=probs_pairs[q])
+            grad_sb = loads.tile([P, PAIR, CLASSES], BF16, tag="grad")
+            nc.sync.dma_start(out=grad_sb[:], in_=grad_pairs[q])
+            rbf_sb = loads.tile([P, PAIR, CLASSES], F32, tag="rbf")
+            nc.sync.dma_start(out=rbf_sb[:], in_=rbf_pairs[q])
+            x_sb = loads.tile([P, PAIR, FEATURES], BF16, tag="x")
+            nc.sync.dma_start(out=x_sb[:], in_=x_pairs[q])
+
+            xx = small.tile([P, PAIR], F32, tag="xx")
+            for j in range(PAIR):
+                squares_s = work.tile([P, FEATURES], BF16, tag="unread_s")
+                nc.scalar.activation(out=squares_s[:], in_=x_sb[:, j, :], func=ACT.Square, accum_out=xx[:, j : j + 1])
+            xx_floor = small.tile([P, PAIR], F32, tag="xx_floor")
+            nc.gpsimd.tensor_scalar_max(out=xx_floor[:], in0=xx[:], scalar1=EPS)
+            inv_xx = small.tile([P, PAIR], F32, tag="inv_xx")
+            nc.vector.reciprocal(out=inv_xx[:], in_=xx_floor[:])
+            rx = small.tile([P, PAIR], F32, tag="rx")
+            nc.scalar.activation(out=rx[:], in_=inv_xx[:], func=ACT.Sqrt)
+
+            r = work.tile([P, PASSES, PACK, PAIR * P], F32, tag="r", bufs=2)
+            for g in range(PASSES):
+                for t0 in range(0, PACK, 2):
+                    rbf_turned = psum_rbf.tile([P, 2, PAIR * P], F32, tag="rbf_turned")
+                    for h in range(2):
+                        c0 = g * K_PASS + (t0 + h) * P
+                        for j in range(PAIR):
+                            nc.tensor.transpose(
+                                rbf_turned[:, h, j * P : (j + 1) * P], rbf_sb[:, j, c0 : c0 + P], ident_f32[:]
+                            )
+                    for h in range(2):
+                        nc.scalar.activation(
+                            out=r[:, g, t0 + h, :],
+                            in_=rbf_turned[:, h, :],
+                            func=ACT.Copy,
+                            scale=rk10[g][:, t0 + h : t0 + h + 1],
+                        )
+
+            out_sb = work.tile([P, PAIR, FEATURES], F32, tag="out")
+            for j in range(PAIR):
+                t_sb = work.tile([P, CLASSES], F32, tag="t")
+                row_sum = small.tile([P, 1], F32, tag="row_sum")
+                nc.vector.scalar_tensor_tensor(
+                    out=t_sb[:],
+                    in0=grad_sb[:, j, :],
+                    scalar=1.0,
+                    in1=probs_sb[:, j, :],
+                    op0=ALU.mult,
+                    op1=ALU.mult,
+                    accum_out=row_sum[:],
+                )
+                neg_sum = small.tile([P, 1], F32, tag="neg_sum")
+                nc.gpsimd.tensor_scalar(
+                    out=neg_sum[:], in0=row_sum[:], scalar1=-1.0, scalar2=0.0, op0=ALU.mult, op1=ALU.add
+                )
+                m_sb = work.tile([P, CLASSES], F32, tag="m")
+                nc.scalar.activation(out=m_sb[:], in_=probs_sb[:, j, :], func=ACT.Copy, scale=neg_sum[:])
+
+                dk_grouped = work.tile([P, PASSES, P, PACK], BF16, tag="dk_grouped", align_bytes=64)
+                for g in range(PASSES):
+                    dl_turned = psum_dl.tile([P, PACK, P], F32, tag="dl_turned")
+                    for t in range(PACK):
+                        c0 = g * K_PASS + t * P
+                        nc.tensor.matmul(
+                            out=dl_turned[:, t, :],
+                            lhsT=t_sb[:, c0 : c0 + P],
+                            rhs=ident_f32[:],
+                            is_transpose=True,
+                            start=True,
+                            stop=False,
+                        )
+                        nc.tensor.matmul(
+                            out=dl_turned[:, t, :],
+                            lhsT=m_sb[:, c0 : c0 + P],
+                            rhs=ident_f32[:],
+                            is_transpose=True,
+                            start=False,
+                            stop=True,
+                        )
+                    nc.vector.tensor_tensor(
+                        out=dk_grouped[:, g, :, :],
+                        in0=dl_turned[:].rearrange("p t b -> p b t"),
+                        in1=r[:, g, :, j * P : (j + 1) * P].rearrange("p t b -> p b t"),
+                        op=ALU.mult,
+                    )
+                dk_codes = work.tile([P, PASSES * P], U32, tag="dk_codes", align_bytes=64)
+                dk_scales = work.tile([P, PASSES * P], U8, tag="dk_scales", align_bytes=64)
+                nc.vector.quantize_mx(
+                    out=dk_codes[:].bitcast(E5M2X4),
+                    scales=dk_scales[:],
+                    in_=dk_grouped[:].rearrange("p g b t -> p (g b t)"),
+                )
+
+                de = [psum_de.tile([P, N_COLS], F32, tag="de", name="de%d" % n) for n in range(N_HALVES)]
+                for g in range(PASSES):
+                    for n in range(N_HALVES):
+                        nc.tensor.matmul_mx(
+                            out=de[n][:],
+                            lhsT=dk_codes[:, g * P : (g + 1) * P].bitcast(E5M2X4),
+                            lhsT_scale=dk_scales[:, g * P : (g + 1) * P],
+                            rhs=k_codes[:, g, n * N_COLS : (n + 1) * N_COLS].bitcast(E4M3X4),
+                            rhs_scale=k_scales[:, g, n * N_COLS : (n + 1) * N_COLS],
+                            start=(g == 0),
+                            stop=(g == PASSES - 1),
+                        )
+
+                for n in range(N_HALVES):
+                    nc.scalar.activation(
+                        out=out_sb[:, j, n * N_COLS : (n + 1) * N_COLS],
+                        in_=de[n][:],
+                        func=ACT.Copy,
+                        scale=rx[:, j : j + 1],
+                    )
+                products = work.tile([P, FEATURES], BF16, tag="unread_v")
+                ux = small.tile([P, 1], F32, tag="ux")
+                nc.vector.scalar_tensor_tensor(
+                    out=products[:],
+                    in0=out_sb[:, j, :],
+                    scalar=1.0,
+                    in1=x_sb[:, j, :],
+                    op0=ALU.mult,
+                    op1=ALU.mult,
+                    accum_out=ux[:],
+                )
+                pull = small.tile([P, 1], F32, tag="pull")
+                nc.vector.tensor_scalar(
+                    out=pull[:], in0=ux[:], scalar1=inv_xx[:, j : j + 1], scalar2=-1.0, op0=ALU.mult, op1=ALU.mult
+                )
+                nc.vector.scalar_tensor_tensor(
+                    out=out_sb[:, j, :],
+                    in0=x_sb[:, j, :],
+                    scalar=pull[:],
+                    in1=out_sb[:, j, :],
+                    op0=ALU.mult,
+                    op1=ALU.add,
+                )
+            nc.gpsimd.dma_start(out=out_pairs[q], in_=out_sb[:])

@@ -21,6 +21,7 @@ N_COLS = 512
 N_HALVES = FEATURES // N_COLS
 PAIR = 2
 PAIRS = TOKENS // (PAIR * P)
+TILES = TOKENS // P
 D_TILES = FEATURES // P
 EPS = 1e-12
 LOGIT_SLOPE = 100.0 * 2.0 / 20.0
@@ -42,14 +43,15 @@ def tile_rbf_softmax_layer_t_v_kernel(tc, x, kernel, rbf, probs, grad_out, out):
         by_pairs(out),
     )
 
-    with ExitStack() as pools:
-        keep = pools.enter_context(tc.tile_pool(name="keep", bufs=1))
-        loads = pools.enter_context(tc.tile_pool(name="loads", bufs=3))
-        work = pools.enter_context(tc.tile_pool(name="work", bufs=3))
-        small = pools.enter_context(tc.tile_pool(name="small", bufs=4))
-        psum_dl = pools.enter_context(tc.psum_pool(name="psum_dl", bufs=2))
-        psum_rbf = pools.enter_context(tc.psum_pool(name="psum_rbf", bufs=2))
-        psum_de = pools.enter_context(tc.psum_pool(name="psum_de", bufs=4))
+    with ExitStack() as stack:
+        keep = stack.enter_context(tc.tile_pool(name="keep", bufs=1))
+        loads = stack.enter_context(tc.tile_pool(name="loads", bufs=3))
+        work = stack.enter_context(tc.tile_pool(name="work", bufs=3))
+        small = stack.enter_context(tc.tile_pool(name="small", bufs=8))
+        psum_dl = stack.enter_context(tc.psum_pool(name="psum_dl", bufs=2))
+        psum_rbf = stack.enter_context(tc.psum_pool(name="psum_rbf", bufs=2))
+        psum_de = stack.enter_context(tc.psum_pool(name="psum_de", bufs=4))
+        stack.enter_context(tc.manual_schedule())
 
         ident_f32 = keep.tile([P, P], F32)
         make_identity(nc, ident_f32[:])
@@ -79,15 +81,6 @@ def tile_rbf_softmax_layer_t_v_kernel(tc, x, kernel, rbf, probs, grad_out, out):
                 nc.vector.tensor_copy(out=grouped_view, in_=turned_view)
             else:
                 nc.scalar.copy(out=grouped_view, in_=turned_view)
-
-        k_codes = keep.tile([P, PASSES, FEATURES], U32, align_bytes=64)
-        k_scales = keep.tile([P, PASSES, FEATURES], U8, align_bytes=64)
-        for g in range(PASSES):
-            nc.vector.quantize_mx(
-                out=k_codes[:, g, :].bitcast(E4M3X4),
-                scales=k_scales[:, g, :],
-                in_=k_grouped[:, g, :, :].rearrange("p d t -> p (d t)"),
-            )
 
         k_sumsq = [keep.tile([P, PACK], F32, name="k_sumsq%d" % g) for g in range(PASSES)]
         for t in range(PACK):
@@ -130,141 +123,203 @@ def tile_rbf_softmax_layer_t_v_kernel(tc, x, kernel, rbf, probs, grad_out, out):
             nc.vector.tensor_tensor(out=rk10_g[:], in0=y[:], in1=step[:], op=ALU.mult)
             rk10.append(rk10_g)
 
-        for q in range(PAIRS):
+        k_codes = keep.tile([P, PASSES, FEATURES], U32, align_bytes=64)
+        k_scales = keep.tile([P, PASSES, FEATURES], U8, align_bytes=64)
+        for g in range(PASSES):
+            nc.vector.quantize_mx(
+                out=k_codes[:, g, :].bitcast(E4M3X4),
+                scales=k_scales[:, g, :],
+                in_=k_grouped[:, g, :, :].rearrange("p d t -> p (d t)"),
+            )
+
+        inputs, t_of, m_of, r_of, dl_of, dk_of, de_of, out_of = {}, {}, {}, {}, {}, {}, {}, {}
+        xx_floor_of, inv_xx_of, rx_of, ux_of, pull_of = {}, {}, {}, {}, {}
+
+        def load_pair(q):
             probs_sb = loads.tile([P, PAIR, CLASSES], F32, tag="probs")
             nc.sync.dma_start(out=probs_sb[:], in_=probs_pairs[q])
             grad_sb = loads.tile([P, PAIR, CLASSES], BF16, tag="grad")
             nc.sync.dma_start(out=grad_sb[:], in_=grad_pairs[q])
             rbf_sb = loads.tile([P, PAIR, CLASSES], F32, tag="rbf")
             nc.sync.dma_start(out=rbf_sb[:], in_=rbf_pairs[q])
-            x_sb = loads.tile([P, PAIR, FEATURES], BF16, tag="x")
+            x_sb = loads.tile([P, PAIR, FEATURES], BF16, tag="x", bufs=5)
             nc.sync.dma_start(out=x_sb[:], in_=x_pairs[q])
+            inputs[q] = {"probs": probs_sb, "grad": grad_sb, "rbf": rbf_sb, "x": x_sb}
 
-            xx = small.tile([P, PAIR], F32, tag="xx")
-            for j in range(PAIR):
-                squares_s = work.tile([P, FEATURES], BF16, tag="unread_s")
-                nc.scalar.activation(out=squares_s[:], in_=x_sb[:, j, :], func=ACT.Square, accum_out=xx[:, j : j + 1])
-            xx_floor = small.tile([P, PAIR], F32, tag="xx_floor")
+        def front(k):
+            q, j = divmod(k, PAIR)
+            t_sb = work.tile([P, CLASSES], F32, tag="t")
+            row_sum = small.tile([P, 1], F32, tag="row_sum")
+            nc.vector.scalar_tensor_tensor(
+                out=t_sb[:],
+                in0=inputs[q]["grad"][:, j, :],
+                scalar=1.0,
+                in1=inputs[q]["probs"][:, j, :],
+                op0=ALU.mult,
+                op1=ALU.mult,
+                accum_out=row_sum[:],
+            )
+            neg_sum = small.tile([P, 1], F32, tag="neg_sum")
+            nc.gpsimd.tensor_scalar(
+                out=neg_sum[:], in0=row_sum[:], scalar1=-1.0, scalar2=0.0, op0=ALU.mult, op1=ALU.add
+            )
+            m_sb = work.tile([P, CLASSES], F32, tag="m")
+            nc.scalar.activation(out=m_sb[:], in_=inputs[q]["probs"][:, j, :], func=ACT.Copy, scale=neg_sum[:])
+            t_of[k], m_of[k] = t_sb, m_sb
+
+        def x_sum_of_squares(k):
+            q, j = divmod(k, PAIR)
+            squares = work.tile([P, FEATURES], BF16, tag="unread_s")
+            xx = small.tile([P, 1], F32, tag="xx")
+            nc.scalar.activation(out=squares[:], in_=inputs[q]["x"][:, j, :], func=ACT.Square, accum_out=xx[:])
+            xx_floor = small.tile([P, 1], F32, tag="xx_floor")
             nc.gpsimd.tensor_scalar_max(out=xx_floor[:], in0=xx[:], scalar1=EPS)
-            inv_xx = small.tile([P, PAIR], F32, tag="inv_xx")
-            nc.vector.reciprocal(out=inv_xx[:], in_=xx_floor[:])
-            rx = small.tile([P, PAIR], F32, tag="rx")
+            xx_floor_of[k] = xx_floor
+
+        def x_reciprocal_length(k):
+            inv_xx = small.tile([P, 1], F32, tag="inv_xx")
+            nc.vector.reciprocal(out=inv_xx[:], in_=xx_floor_of[k][:])
+            rx = small.tile([P, 1], F32, tag="rx")
             nc.scalar.activation(out=rx[:], in_=inv_xx[:], func=ACT.Sqrt)
+            inv_xx_of[k], rx_of[k] = inv_xx, rx
 
-            r = work.tile([P, PASSES, PACK, PAIR * P], F32, tag="r", bufs=2)
-            for g in range(PASSES):
-                for t0 in range(0, PACK, 2):
-                    rbf_turned = psum_rbf.tile([P, 2, PAIR * P], F32, tag="rbf_turned")
-                    for h in range(2):
-                        c0 = g * K_PASS + (t0 + h) * P
-                        for j in range(PAIR):
-                            nc.tensor.transpose(
-                                rbf_turned[:, h, j * P : (j + 1) * P], rbf_sb[:, j, c0 : c0 + P], ident_f32[:]
-                            )
-                    for h in range(2):
-                        nc.scalar.activation(
-                            out=r[:, g, t0 + h, :],
-                            in_=rbf_turned[:, h, :],
-                            func=ACT.Copy,
-                            scale=rk10[g][:, t0 + h : t0 + h + 1],
-                        )
-
-            out_sb = work.tile([P, PAIR, FEATURES], F32, tag="out")
-            for j in range(PAIR):
-                t_sb = work.tile([P, CLASSES], F32, tag="t")
-                row_sum = small.tile([P, 1], F32, tag="row_sum")
-                nc.vector.scalar_tensor_tensor(
-                    out=t_sb[:],
-                    in0=grad_sb[:, j, :],
-                    scalar=1.0,
-                    in1=probs_sb[:, j, :],
-                    op0=ALU.mult,
-                    op1=ALU.mult,
-                    accum_out=row_sum[:],
-                )
-                neg_sum = small.tile([P, 1], F32, tag="neg_sum")
-                nc.gpsimd.tensor_scalar(
-                    out=neg_sum[:], in0=row_sum[:], scalar1=-1.0, scalar2=0.0, op0=ALU.mult, op1=ALU.add
-                )
-                m_sb = work.tile([P, CLASSES], F32, tag="m")
-                nc.scalar.activation(out=m_sb[:], in_=probs_sb[:, j, :], func=ACT.Copy, scale=neg_sum[:])
-
-                dk_grouped = work.tile([P, PASSES, P, PACK], BF16, tag="dk_grouped", align_bytes=64)
-                for g in range(PASSES):
-                    dl_turned = psum_dl.tile([P, PACK, P], F32, tag="dl_turned")
-                    for t in range(PACK):
-                        c0 = g * K_PASS + t * P
-                        nc.tensor.matmul(
-                            out=dl_turned[:, t, :],
-                            lhsT=t_sb[:, c0 : c0 + P],
-                            rhs=ident_f32[:],
-                            is_transpose=True,
-                            start=True,
-                            stop=False,
-                        )
-                        nc.tensor.matmul(
-                            out=dl_turned[:, t, :],
-                            lhsT=m_sb[:, c0 : c0 + P],
-                            rhs=ident_f32[:],
-                            is_transpose=True,
-                            start=False,
-                            stop=True,
-                        )
-                    nc.vector.tensor_tensor(
-                        out=dk_grouped[:, g, :, :],
-                        in0=dl_turned[:].rearrange("p t b -> p b t"),
-                        in1=r[:, g, :, j * P : (j + 1) * P].rearrange("p t b -> p b t"),
-                        op=ALU.mult,
+        def turn_rbf(q, g, t0):
+            if (g, t0) == (0, 0):
+                r_of[q] = work.tile([P, PASSES, PACK, PAIR * P], F32, tag="r", bufs=2, name="r")
+            rbf_turned = psum_rbf.tile([P, 2, PAIR * P], F32, tag="rbf_turned")
+            for h in range(2):
+                c0 = g * K_PASS + (t0 + h) * P
+                for j in range(PAIR):
+                    nc.tensor.transpose(
+                        rbf_turned[:, h, j * P : (j + 1) * P], inputs[q]["rbf"][:, j, c0 : c0 + P], ident_f32[:]
                     )
-                dk_codes = work.tile([P, PASSES * P], U32, tag="dk_codes", align_bytes=64)
-                dk_scales = work.tile([P, PASSES * P], U8, tag="dk_scales", align_bytes=64)
-                nc.vector.quantize_mx(
-                    out=dk_codes[:].bitcast(E5M2X4),
-                    scales=dk_scales[:],
-                    in_=dk_grouped[:].rearrange("p g b t -> p (g b t)"),
+            for h in range(2):
+                nc.scalar.activation(
+                    out=r_of[q][:, g, t0 + h, :],
+                    in_=rbf_turned[:, h, :],
+                    func=ACT.Copy,
+                    scale=rk10[g][:, t0 + h : t0 + h + 1],
                 )
 
-                de = [psum_de.tile([P, N_COLS], F32, tag="de", name="de%d" % n) for n in range(N_HALVES)]
-                for g in range(PASSES):
-                    for n in range(N_HALVES):
-                        nc.tensor.matmul_mx(
-                            out=de[n][:],
-                            lhsT=dk_codes[:, g * P : (g + 1) * P].bitcast(E5M2X4),
-                            lhsT_scale=dk_scales[:, g * P : (g + 1) * P],
-                            rhs=k_codes[:, g, n * N_COLS : (n + 1) * N_COLS].bitcast(E4M3X4),
-                            rhs_scale=k_scales[:, g, n * N_COLS : (n + 1) * N_COLS],
-                            start=(g == 0),
-                            stop=(g == PASSES - 1),
-                        )
+        def turn_dl(k, g):
+            dl_turned = psum_dl.tile([P, PACK, P], F32, tag="dl_turned")
+            for t in range(PACK):
+                c0 = g * K_PASS + t * P
+                nc.tensor.matmul(
+                    out=dl_turned[:, t, :],
+                    lhsT=t_of[k][:, c0 : c0 + P],
+                    rhs=ident_f32[:],
+                    is_transpose=True,
+                    start=True,
+                    stop=False,
+                )
+                nc.tensor.matmul(
+                    out=dl_turned[:, t, :],
+                    lhsT=m_of[k][:, c0 : c0 + P],
+                    rhs=ident_f32[:],
+                    is_transpose=True,
+                    start=False,
+                    stop=True,
+                )
+            dl_of[k, g] = dl_turned
 
-                for n in range(N_HALVES):
-                    nc.scalar.activation(
-                        out=out_sb[:, j, n * N_COLS : (n + 1) * N_COLS],
-                        in_=de[n][:],
-                        func=ACT.Copy,
-                        scale=rx[:, j : j + 1],
-                    )
-                products = work.tile([P, FEATURES], BF16, tag="unread_v")
-                ux = small.tile([P, 1], F32, tag="ux")
-                nc.vector.scalar_tensor_tensor(
-                    out=products[:],
-                    in0=out_sb[:, j, :],
-                    scalar=1.0,
-                    in1=x_sb[:, j, :],
-                    op0=ALU.mult,
-                    op1=ALU.mult,
-                    accum_out=ux[:],
+        def scale_dk(k, g):
+            q, j = divmod(k, PAIR)
+            dk_grouped = work.tile([P, P, PACK], BF16, tag="dk_grouped", bufs=4, align_bytes=64)
+            nc.vector.tensor_tensor(
+                out=dk_grouped[:],
+                in0=dl_of[k, g][:].rearrange("p t b -> p b t"),
+                in1=r_of[q][:, g, :, j * P : (j + 1) * P].rearrange("p t b -> p b t"),
+                op=ALU.mult,
+            )
+            dk_of[k, g] = dk_grouped
+
+        def quantise_and_multiply(k, g):
+            dk_codes = work.tile([P, P], U32, tag="dk_codes", bufs=4, align_bytes=64)
+            dk_scales = work.tile([P, P], U8, tag="dk_scales", bufs=4, align_bytes=64)
+            nc.vector.quantize_mx(
+                out=dk_codes[:].bitcast(E5M2X4),
+                scales=dk_scales[:],
+                in_=dk_of[k, g][:].rearrange("p b t -> p (b t)"),
+            )
+            if g == 0:
+                de_of[k] = [psum_de.tile([P, N_COLS], F32, tag="de", name="de%d" % n) for n in range(N_HALVES)]
+            for n in range(N_HALVES):
+                nc.tensor.matmul_mx(
+                    out=de_of[k][n][:],
+                    lhsT=dk_codes[:].bitcast(E5M2X4),
+                    lhsT_scale=dk_scales[:],
+                    rhs=k_codes[:, g, n * N_COLS : (n + 1) * N_COLS].bitcast(E4M3X4),
+                    rhs_scale=k_scales[:, g, n * N_COLS : (n + 1) * N_COLS],
+                    start=(g == 0),
+                    stop=(g == PASSES - 1),
                 )
-                pull = small.tile([P, 1], F32, tag="pull")
-                nc.vector.tensor_scalar(
-                    out=pull[:], in0=ux[:], scalar1=inv_xx[:, j : j + 1], scalar2=-1.0, op0=ALU.mult, op1=ALU.mult
+
+        def leave_psum(k):
+            out_sb = work.tile([P, FEATURES], F32, tag="out", bufs=4)
+            for n in range(N_HALVES):
+                nc.scalar.activation(
+                    out=out_sb[:, n * N_COLS : (n + 1) * N_COLS], in_=de_of[k][n][:], func=ACT.Copy, scale=rx_of[k][:]
                 )
-                nc.vector.scalar_tensor_tensor(
-                    out=out_sb[:, j, :],
-                    in0=x_sb[:, j, :],
-                    scalar=pull[:],
-                    in1=out_sb[:, j, :],
-                    op0=ALU.mult,
-                    op1=ALU.add,
-                )
-            nc.gpsimd.dma_start(out=out_pairs[q], in_=out_sb[:])
+            out_of[k] = out_sb
+
+        def dot_with_x(k):
+            q, j = divmod(k, PAIR)
+            products = work.tile([P, FEATURES], BF16, tag="unread_v")
+            ux = small.tile([P, 1], F32, tag="ux")
+            nc.vector.scalar_tensor_tensor(
+                out=products[:],
+                in0=out_of[k][:],
+                scalar=1.0,
+                in1=inputs[q]["x"][:, j, :],
+                op0=ALU.mult,
+                op1=ALU.mult,
+                accum_out=ux[:],
+            )
+            ux_of[k] = ux
+
+        def pull_factor(k):
+            pull = small.tile([P, 1], F32, tag="pull")
+            nc.vector.tensor_scalar(
+                out=pull[:], in0=ux_of[k][:], scalar1=inv_xx_of[k][:], scalar2=-1.0, op0=ALU.mult, op1=ALU.mult
+            )
+            pull_of[k] = pull
+
+        def project_and_store(k):
+            q, j = divmod(k, PAIR)
+            nc.vector.scalar_tensor_tensor(
+                out=out_of[k][:],
+                in0=inputs[q]["x"][:, j, :],
+                scalar=pull_of[k][:],
+                in1=out_of[k][:],
+                op0=ALU.mult,
+                op1=ALU.add,
+            )
+            nc.gpsimd.dma_start(out=out_pairs[q][:, j, :], in_=out_of[k][:])
+
+        def if_tile(stage, k, *more):
+            if 0 <= k < TILES:
+                stage(k, *more)
+
+        load_pair(0)
+        load_pair(1)
+        for s in range(TILES + 4):
+            if s % PAIR == 0 and s // PAIR + 2 < PAIRS:
+                load_pair(s // PAIR + 2)
+            if_tile(leave_psum, s - 3)
+            if_tile(scale_dk, s - 2, 0)
+            if_tile(turn_dl, s - 1, 0)
+            if s < TILES:
+                turn_rbf(s // PAIR, s % PAIR, 0)
+            if_tile(dot_with_x, s - 4)
+            if_tile(quantise_and_multiply, s - 2, 0)
+            if_tile(scale_dk, s - 2, 1)
+            if_tile(turn_dl, s - 1, 1)
+            if_tile(x_sum_of_squares, s - 1)
+            if s < TILES:
+                turn_rbf(s // PAIR, s % PAIR, 2)
+            if_tile(pull_factor, s - 4)
+            if_tile(x_reciprocal_length, s - 2)
+            if_tile(front, s)
+            if_tile(quantise_and_multiply, s - 2, 1)
+            if_tile(project_and_store, s - 4)

@@ -134,6 +134,7 @@ def tile_rbf_softmax_layer_t_v_kernel(tc, x, kernel, rbf, probs, grad_out, out):
 
         inputs, t_of, m_of, r_of, dl_of, dk_of, de_of, out_of = {}, {}, {}, {}, {}, {}, {}, {}
         xx_floor_of, inv_xx_of, rx_of, ux_of, pull_of = {}, {}, {}, {}, {}
+        x_of, neg_sum_of, rbf_turned_of = {}, {}, {}
 
         def load_pair(q):
             probs_sb = loads.tile([P, PAIR, CLASSES], F32, tag="probs")
@@ -142,13 +143,16 @@ def tile_rbf_softmax_layer_t_v_kernel(tc, x, kernel, rbf, probs, grad_out, out):
             nc.sync.dma_start(out=grad_sb[:], in_=grad_pairs[q])
             rbf_sb = loads.tile([P, PAIR, CLASSES], F32, tag="rbf")
             nc.sync.dma_start(out=rbf_sb[:], in_=rbf_pairs[q])
+            inputs[q] = {"probs": probs_sb, "grad": grad_sb, "rbf": rbf_sb}
+
+        def load_x(q):
             x_sb = loads.tile([P, PAIR, FEATURES], BF16, tag="x", bufs=5)
             nc.sync.dma_start(out=x_sb[:], in_=x_pairs[q])
-            inputs[q] = {"probs": probs_sb, "grad": grad_sb, "rbf": rbf_sb, "x": x_sb}
+            x_of[q] = x_sb
 
         def front(k):
             q, j = divmod(k, PAIR)
-            t_sb = work.tile([P, CLASSES], F32, tag="t")
+            t_sb = work.tile([P, CLASSES], F32, tag="t", bufs=4)
             row_sum = small.tile([P, 1], F32, tag="row_sum")
             nc.vector.scalar_tensor_tensor(
                 out=t_sb[:],
@@ -163,15 +167,19 @@ def tile_rbf_softmax_layer_t_v_kernel(tc, x, kernel, rbf, probs, grad_out, out):
             nc.gpsimd.tensor_scalar(
                 out=neg_sum[:], in0=row_sum[:], scalar1=-1.0, scalar2=0.0, op0=ALU.mult, op1=ALU.add
             )
+            t_of[k], neg_sum_of[k] = t_sb, neg_sum
+
+        def minus_sum_probs(k):
+            q, j = divmod(k, PAIR)
             m_sb = work.tile([P, CLASSES], F32, tag="m")
-            nc.scalar.activation(out=m_sb[:], in_=inputs[q]["probs"][:, j, :], func=ACT.Copy, scale=neg_sum[:])
-            t_of[k], m_of[k] = t_sb, m_sb
+            nc.scalar.activation(out=m_sb[:], in_=inputs[q]["probs"][:, j, :], func=ACT.Copy, scale=neg_sum_of[k][:])
+            m_of[k] = m_sb
 
         def x_sum_of_squares(k):
             q, j = divmod(k, PAIR)
             squares = work.tile([P, FEATURES], BF16, tag="unread_s")
             xx = small.tile([P, 1], F32, tag="xx")
-            nc.scalar.activation(out=squares[:], in_=inputs[q]["x"][:, j, :], func=ACT.Square, accum_out=xx[:])
+            nc.scalar.activation(out=squares[:], in_=x_of[q][:, j, :], func=ACT.Square, accum_out=xx[:])
             xx_floor = small.tile([P, 1], F32, tag="xx_floor")
             nc.gpsimd.tensor_scalar_max(out=xx_floor[:], in0=xx[:], scalar1=EPS)
             xx_floor_of[k] = xx_floor
@@ -184,8 +192,6 @@ def tile_rbf_softmax_layer_t_v_kernel(tc, x, kernel, rbf, probs, grad_out, out):
             inv_xx_of[k], rx_of[k] = inv_xx, rx
 
         def turn_rbf(q, g, t0):
-            if (g, t0) == (0, 0):
-                r_of[q] = work.tile([P, PASSES, PACK, PAIR * P], F32, tag="r", bufs=2, name="r")
             rbf_turned = psum_rbf.tile([P, 2, PAIR * P], F32, tag="rbf_turned")
             for h in range(2):
                 c0 = g * K_PASS + (t0 + h) * P
@@ -193,10 +199,15 @@ def tile_rbf_softmax_layer_t_v_kernel(tc, x, kernel, rbf, probs, grad_out, out):
                     nc.tensor.transpose(
                         rbf_turned[:, h, j * P : (j + 1) * P], inputs[q]["rbf"][:, j, c0 : c0 + P], ident_f32[:]
                     )
+            rbf_turned_of[q, g, t0] = rbf_turned
+
+        def scale_rbf(q, g, t0):
+            if (g, t0) == (0, 0):
+                r_of[q] = work.tile([P, PASSES, PACK, PAIR * P], F32, tag="r", name="r")
             for h in range(2):
                 nc.scalar.activation(
                     out=r_of[q][:, g, t0 + h, :],
-                    in_=rbf_turned[:, h, :],
+                    in_=rbf_turned_of[q, g, t0][:, h, :],
                     func=ACT.Copy,
                     scale=rk10[g][:, t0 + h : t0 + h + 1],
                 )
@@ -271,7 +282,7 @@ def tile_rbf_softmax_layer_t_v_kernel(tc, x, kernel, rbf, probs, grad_out, out):
                 out=products[:],
                 in0=out_of[k][:],
                 scalar=1.0,
-                in1=inputs[q]["x"][:, j, :],
+                in1=x_of[q][:, j, :],
                 op0=ALU.mult,
                 op1=ALU.mult,
                 accum_out=ux[:],
@@ -289,7 +300,7 @@ def tile_rbf_softmax_layer_t_v_kernel(tc, x, kernel, rbf, probs, grad_out, out):
             q, j = divmod(k, PAIR)
             nc.vector.scalar_tensor_tensor(
                 out=out_of[k][:],
-                in0=inputs[q]["x"][:, j, :],
+                in0=x_of[q][:, j, :],
                 scalar=pull_of[k][:],
                 in1=out_of[k][:],
                 op0=ALU.mult,
@@ -301,25 +312,33 @@ def tile_rbf_softmax_layer_t_v_kernel(tc, x, kernel, rbf, probs, grad_out, out):
             if 0 <= k < TILES:
                 stage(k, *more)
 
+        def if_step(stage, s, t0):
+            if 0 <= s < TILES:
+                stage(s // PAIR, s % PAIR, t0)
+
         load_pair(0)
+        load_x(0)
         load_pair(1)
-        for s in range(TILES + 4):
+        for s in range(TILES + 5):
+            if s % PAIR == 0 and s // PAIR + 1 < PAIRS:
+                load_x(s // PAIR + 1)
             if s % PAIR == 0 and s // PAIR + 2 < PAIRS:
                 load_pair(s // PAIR + 2)
-            if_tile(leave_psum, s - 3)
-            if_tile(scale_dk, s - 2, 0)
-            if_tile(turn_dl, s - 1, 0)
-            if s < TILES:
-                turn_rbf(s // PAIR, s % PAIR, 0)
-            if_tile(dot_with_x, s - 4)
-            if_tile(quantise_and_multiply, s - 2, 0)
-            if_tile(scale_dk, s - 2, 1)
-            if_tile(turn_dl, s - 1, 1)
-            if_tile(x_sum_of_squares, s - 1)
-            if s < TILES:
-                turn_rbf(s // PAIR, s % PAIR, 2)
-            if_tile(pull_factor, s - 4)
-            if_tile(x_reciprocal_length, s - 2)
+            if_tile(leave_psum, s - 4)
+            if_tile(scale_dk, s - 3, 0)
+            if_tile(turn_dl, s - 2, 0)
+            if_step(scale_rbf, s - 1, 2)
+            if_tile(dot_with_x, s - 5)
+            if_step(turn_rbf, s, 0)
+            if_tile(quantise_and_multiply, s - 3, 0)
+            if_tile(x_sum_of_squares, s - 2)
+            if_tile(scale_dk, s - 3, 1)
+            if_tile(turn_dl, s - 2, 1)
+            if_tile(pull_factor, s - 5)
+            if_step(scale_rbf, s, 0)
+            if_tile(x_reciprocal_length, s - 3)
             if_tile(front, s)
-            if_tile(quantise_and_multiply, s - 2, 1)
-            if_tile(project_and_store, s - 4)
+            if_tile(quantise_and_multiply, s - 3, 1)
+            if_tile(minus_sum_probs, s - 1)
+            if_step(turn_rbf, s, 2)
+            if_tile(project_and_store, s - 5)

@@ -48,9 +48,9 @@ def tile_rbf_softmax_layer_t_v_kernel(tc, x, kernel, rbf, probs, grad_out, out):
         loads = stack.enter_context(tc.tile_pool(name="loads", bufs=3))
         work = stack.enter_context(tc.tile_pool(name="work", bufs=3))
         small = stack.enter_context(tc.tile_pool(name="small", bufs=8))
-        psum_dl = stack.enter_context(tc.psum_pool(name="psum_dl", bufs=2))
+        psum_dl = stack.enter_context(tc.psum_pool(name="psum_dl", bufs=4))
         psum_rbf = stack.enter_context(tc.psum_pool(name="psum_rbf", bufs=2))
-        psum_de = stack.enter_context(tc.psum_pool(name="psum_de", bufs=4))
+        psum_de = stack.enter_context(tc.psum_pool(name="psum_de", bufs=2))
         stack.enter_context(tc.manual_schedule())
 
         ident_f32 = keep.tile([P, P], F32)
@@ -70,7 +70,7 @@ def tile_rbf_softmax_layer_t_v_kernel(tc, x, kernel, rbf, probs, grad_out, out):
             )
         k_grouped = keep.tile([P, PASSES, FEATURES, PACK], BF16, align_bytes=64)
         for i in range(D_TILES):
-            k_turned = psum_de.tile([P, PASSES, PACK, P], BF16, tag="de")
+            k_turned = psum_dl.tile([P, PASSES, PACK, P], BF16, tag="dl_turned")
             for g in range(PASSES):
                 for t in range(PACK):
                     c0 = g * K_PASS + t * P
@@ -203,7 +203,7 @@ def tile_rbf_softmax_layer_t_v_kernel(tc, x, kernel, rbf, probs, grad_out, out):
 
         def scale_rbf(q, g, t0):
             if (g, t0) == (0, 0):
-                r_of[q] = work.tile([P, PASSES, PACK, PAIR * P], F32, tag="r", name="r")
+                r_of[q] = work.tile([P, PASSES, PACK, PAIR * P], F32, tag="r", bufs=2, name="r")
             for h in range(2):
                 nc.scalar.activation(
                     out=r_of[q][:, g, t0 + h, :],
@@ -236,35 +236,35 @@ def tile_rbf_softmax_layer_t_v_kernel(tc, x, kernel, rbf, probs, grad_out, out):
 
         def scale_dk(k, g):
             q, j = divmod(k, PAIR)
-            dk_grouped = work.tile([P, P, PACK], BF16, tag="dk_grouped", bufs=4, align_bytes=64)
+            if g == 0:
+                dk_of[k] = work.tile([P, PASSES, P, PACK], BF16, tag="dk_grouped", align_bytes=64, name="dk_grouped")
             nc.vector.tensor_tensor(
-                out=dk_grouped[:],
+                out=dk_of[k][:, g, :, :],
                 in0=dl_of[k, g][:].rearrange("p t b -> p b t"),
                 in1=r_of[q][:, g, :, j * P : (j + 1) * P].rearrange("p t b -> p b t"),
                 op=ALU.mult,
             )
-            dk_of[k, g] = dk_grouped
 
-        def quantise_and_multiply(k, g):
-            dk_codes = work.tile([P, P], U32, tag="dk_codes", bufs=4, align_bytes=64)
-            dk_scales = work.tile([P, P], U8, tag="dk_scales", bufs=4, align_bytes=64)
+        def quantise_and_multiply(k):
+            dk_codes = work.tile([P, PASSES * P], U32, tag="dk_codes", align_bytes=64)
+            dk_scales = work.tile([P, PASSES * P], U8, tag="dk_scales", align_bytes=64)
             nc.vector.quantize_mx(
                 out=dk_codes[:].bitcast(E5M2X4),
                 scales=dk_scales[:],
-                in_=dk_of[k, g][:].rearrange("p b t -> p (b t)"),
+                in_=dk_of[k][:].rearrange("p g b t -> p (g b t)"),
             )
-            if g == 0:
-                de_of[k] = [psum_de.tile([P, N_COLS], F32, tag="de", name="de%d" % n) for n in range(N_HALVES)]
-            for n in range(N_HALVES):
-                nc.tensor.matmul_mx(
-                    out=de_of[k][n][:],
-                    lhsT=dk_codes[:].bitcast(E5M2X4),
-                    lhsT_scale=dk_scales[:],
-                    rhs=k_codes[:, g, n * N_COLS : (n + 1) * N_COLS].bitcast(E4M3X4),
-                    rhs_scale=k_scales[:, g, n * N_COLS : (n + 1) * N_COLS],
-                    start=(g == 0),
-                    stop=(g == PASSES - 1),
-                )
+            de_of[k] = [psum_de.tile([P, N_COLS], F32, tag="de", name="de%d" % n) for n in range(N_HALVES)]
+            for g in range(PASSES):
+                for n in range(N_HALVES):
+                    nc.tensor.matmul_mx(
+                        out=de_of[k][n][:],
+                        lhsT=dk_codes[:, g * P : (g + 1) * P].bitcast(E5M2X4),
+                        lhsT_scale=dk_scales[:, g * P : (g + 1) * P],
+                        rhs=k_codes[:, g, n * N_COLS : (n + 1) * N_COLS].bitcast(E4M3X4),
+                        rhs_scale=k_scales[:, g, n * N_COLS : (n + 1) * N_COLS],
+                        start=(g == 0),
+                        stop=(g == PASSES - 1),
+                    )
 
         def leave_psum(k):
             out_sb = work.tile([P, FEATURES], F32, tag="out", bufs=4)
@@ -324,21 +324,20 @@ def tile_rbf_softmax_layer_t_v_kernel(tc, x, kernel, rbf, probs, grad_out, out):
                 load_x(s // PAIR + 1)
             if s % PAIR == 0 and s // PAIR + 2 < PAIRS:
                 load_pair(s // PAIR + 2)
-            if_tile(leave_psum, s - 4)
-            if_tile(scale_dk, s - 3, 0)
-            if_tile(turn_dl, s - 2, 0)
-            if_step(scale_rbf, s - 1, 2)
-            if_tile(dot_with_x, s - 5)
-            if_step(turn_rbf, s, 0)
-            if_tile(quantise_and_multiply, s - 3, 0)
-            if_tile(x_sum_of_squares, s - 2)
-            if_tile(scale_dk, s - 3, 1)
-            if_tile(turn_dl, s - 2, 1)
-            if_tile(pull_factor, s - 5)
-            if_step(scale_rbf, s, 0)
-            if_tile(x_reciprocal_length, s - 3)
-            if_tile(front, s)
-            if_tile(quantise_and_multiply, s - 3, 1)
             if_tile(minus_sum_probs, s - 1)
+            if_tile(scale_dk, s - 3, 0)
+            if_tile(scale_dk, s - 3, 1)
+            if_step(scale_rbf, s - 1, 0)
+            if_step(scale_rbf, s - 1, 2)
+            if_tile(pull_factor, s - 5)
+            if_tile(x_reciprocal_length, s - 3)
+            if_tile(quantise_and_multiply, s - 3)
+            if_tile(turn_dl, s - 1, 0)
+            if_tile(turn_dl, s - 1, 1)
+            if_step(turn_rbf, s, 0)
             if_step(turn_rbf, s, 2)
             if_tile(project_and_store, s - 5)
+            if_tile(x_sum_of_squares, s - 2)
+            if_tile(front, s)
+            if_tile(leave_psum, s - 3)
+            if_tile(dot_with_x, s - 4)

@@ -48,9 +48,9 @@ def tile_rbf_softmax_layer_t_v_kernel(tc, x, kernel, rbf, probs, grad_out, out):
         loads = stack.enter_context(tc.tile_pool(name="loads", bufs=3))
         work = stack.enter_context(tc.tile_pool(name="work", bufs=3))
         small = stack.enter_context(tc.tile_pool(name="small", bufs=8))
-        psum_dl = stack.enter_context(tc.psum_pool(name="psum_dl", bufs=4))
+        psum_dl = stack.enter_context(tc.psum_pool(name="psum_dl", bufs=2))
         psum_rbf = stack.enter_context(tc.psum_pool(name="psum_rbf", bufs=2))
-        psum_de = stack.enter_context(tc.psum_pool(name="psum_de", bufs=2))
+        psum_de = stack.enter_context(tc.psum_pool(name="psum_de", bufs=4))
         stack.enter_context(tc.manual_schedule())
 
         ident_f32 = keep.tile([P, P], F32)
@@ -69,8 +69,15 @@ def tile_rbf_softmax_layer_t_v_kernel(tc, x, kernel, rbf, probs, grad_out, out):
                 in_=kernel[i * P : (i + 2) * P, :].rearrange("(i p) c -> p i c", p=P),
             )
         k_grouped = keep.tile([P, PASSES, FEATURES, PACK], BF16, align_bytes=64)
-        for i in range(D_TILES):
-            k_turned = psum_dl.tile([P, PASSES, PACK, P], BF16, tag="dl_turned")
+        k_codes = keep.tile([P, PASSES, FEATURES], U32, align_bytes=64)
+        k_scales = keep.tile([P, PASSES, FEATURES], U8, align_bytes=64)
+        k_partial = [keep.tile([P, 2, PACK], F32, name="k_partial%d" % g) for g in range(PASSES)]
+        rk10 = keep.tile([P, PASSES, PACK], F32)
+        k_a = keep.tile([P, PASSES, PACK], F32)
+        k_y = keep.tile([P, PASSES, PACK], F32)
+
+        def turn_kernel(i):
+            k_turned = psum_de.tile([P, PASSES, PACK, P], BF16, tag="de")
             for g in range(PASSES):
                 for t in range(PACK):
                     c0 = g * K_PASS + t * P
@@ -82,50 +89,54 @@ def tile_rbf_softmax_layer_t_v_kernel(tc, x, kernel, rbf, probs, grad_out, out):
             else:
                 nc.scalar.copy(out=grouped_view, in_=turned_view)
 
-        k_sumsq = [keep.tile([P, PACK], F32, name="k_sumsq%d" % g) for g in range(PASSES)]
-        for t in range(PACK):
-            squares_s = work.tile([P, FEATURES], BF16, tag="unread_s")
-            nc.scalar.activation(
-                out=squares_s[:], in_=k_grouped[:, 0, :, t], func=ACT.Square, accum_out=k_sumsq[0][:, t : t + 1]
-            )
-            squares_v = work.tile([P, FEATURES], BF16, tag="unread_v")
-            nc.vector.scalar_tensor_tensor(
-                out=squares_v[:],
-                in0=k_grouped[:, 1, :, t],
-                scalar=1.0,
-                in1=k_grouped[:, 1, :, t],
-                op0=ALU.mult,
-                op1=ALU.mult,
-                accum_out=k_sumsq[1][:, t : t + 1],
-            )
-        rk10 = []
-        for g in range(PASSES):
-            a = keep.tile([P, PACK], F32, name="k_a%d" % g)
-            nc.vector.tensor_scalar_max(out=a[:], in0=k_sumsq[g][:], scalar1=EPS)
-            inv_a = keep.tile([P, PACK], F32, name="k_inv_a%d" % g)
-            nc.vector.reciprocal(out=inv_a[:], in_=a[:])
-            y = keep.tile([P, PACK], F32, name="k_y%d" % g)
-            nc.scalar.activation(out=y[:], in_=inv_a[:], func=ACT.Sqrt)
-            yy = keep.tile([P, PACK], F32, name="k_yy%d" % g)
-            nc.vector.tensor_tensor(out=yy[:], in0=y[:], in1=y[:], op=ALU.mult)
-            ayy = keep.tile([P, PACK], F32, name="k_ayy%d" % g)
-            nc.vector.tensor_tensor(out=ayy[:], in0=yy[:], in1=a[:], op=ALU.mult)
-            step = keep.tile([P, PACK], F32, name="k_step%d" % g)
+        def kernel_sums_of_squares(half):
+            d0 = half * (FEATURES // 2)
+            for t in range(PACK):
+                squares_s = work.tile([P, FEATURES // 2], BF16, tag="unread_s")
+                nc.scalar.activation(
+                    out=squares_s[:],
+                    in_=k_grouped[:, 0, d0 : d0 + FEATURES // 2, t],
+                    func=ACT.Square,
+                    accum_out=k_partial[0][:, half, t : t + 1],
+                )
+                squares_v = work.tile([P, FEATURES // 2], BF16, tag="unread_v")
+                nc.vector.scalar_tensor_tensor(
+                    out=squares_v[:],
+                    in0=k_grouped[:, 1, d0 : d0 + FEATURES // 2, t],
+                    scalar=1.0,
+                    in1=k_grouped[:, 1, d0 : d0 + FEATURES // 2, t],
+                    op0=ALU.mult,
+                    op1=ALU.mult,
+                    accum_out=k_partial[1][:, half, t : t + 1],
+                )
+
+        def kernel_table_rsqrt():
+            for g in range(PASSES):
+                nc.vector.tensor_tensor(
+                    out=k_a[:, g, :], in0=k_partial[g][:, 0, :], in1=k_partial[g][:, 1, :], op=ALU.add
+                )
+            nc.vector.tensor_scalar_max(out=k_a[:], in0=k_a[:], scalar1=EPS)
+            inv_a = keep.tile([P, PASSES, PACK], F32)
+            nc.vector.reciprocal(out=inv_a[:], in_=k_a[:])
+            nc.scalar.activation(out=k_y[:], in_=inv_a[:], func=ACT.Sqrt)
+
+        def kernel_newton_step():
+            yy = keep.tile([P, PASSES, PACK], F32)
+            nc.vector.tensor_tensor(out=yy[:], in0=k_y[:], in1=k_y[:], op=ALU.mult)
+            ayy = keep.tile([P, PASSES, PACK], F32)
+            nc.vector.tensor_tensor(out=ayy[:], in0=yy[:], in1=k_a[:], op=ALU.mult)
+            factor = keep.tile([P, PASSES, PACK], F32)
             nc.vector.tensor_scalar(
-                out=step[:],
+                out=factor[:],
                 in0=ayy[:],
                 scalar1=-0.5 * LOGIT_SLOPE,
                 scalar2=1.5 * LOGIT_SLOPE,
                 op0=ALU.mult,
                 op1=ALU.add,
             )
-            rk10_g = keep.tile([P, PACK], F32, name="rk10_%d" % g)
-            nc.vector.tensor_tensor(out=rk10_g[:], in0=y[:], in1=step[:], op=ALU.mult)
-            rk10.append(rk10_g)
+            nc.vector.tensor_tensor(out=rk10[:], in0=k_y[:], in1=factor[:], op=ALU.mult)
 
-        k_codes = keep.tile([P, PASSES, FEATURES], U32, align_bytes=64)
-        k_scales = keep.tile([P, PASSES, FEATURES], U8, align_bytes=64)
-        for g in range(PASSES):
+        def quantise_kernel(g):
             nc.vector.quantize_mx(
                 out=k_codes[:, g, :].bitcast(E4M3X4),
                 scales=k_scales[:, g, :],
@@ -134,7 +145,7 @@ def tile_rbf_softmax_layer_t_v_kernel(tc, x, kernel, rbf, probs, grad_out, out):
 
         inputs, t_of, m_of, r_of, dl_of, dk_of, de_of, out_of = {}, {}, {}, {}, {}, {}, {}, {}
         xx_floor_of, inv_xx_of, rx_of, ux_of, pull_of = {}, {}, {}, {}, {}
-        x_of, neg_sum_of, rbf_turned_of = {}, {}, {}
+        x_of, row_sum_of, neg_sum_of, rbf_turned_of = {}, {}, {}, {}
 
         def load_pair(q):
             probs_sb = loads.tile([P, PAIR, CLASSES], F32, tag="probs")
@@ -152,7 +163,7 @@ def tile_rbf_softmax_layer_t_v_kernel(tc, x, kernel, rbf, probs, grad_out, out):
 
         def front(k):
             q, j = divmod(k, PAIR)
-            t_sb = work.tile([P, CLASSES], F32, tag="t", bufs=4)
+            t_sb = work.tile([P, CLASSES], F32, tag="t", bufs=5)
             row_sum = small.tile([P, 1], F32, tag="row_sum")
             nc.vector.scalar_tensor_tensor(
                 out=t_sb[:],
@@ -163,16 +174,30 @@ def tile_rbf_softmax_layer_t_v_kernel(tc, x, kernel, rbf, probs, grad_out, out):
                 op1=ALU.mult,
                 accum_out=row_sum[:],
             )
-            neg_sum = small.tile([P, 1], F32, tag="neg_sum")
-            nc.gpsimd.tensor_scalar(
-                out=neg_sum[:], in0=row_sum[:], scalar1=-1.0, scalar2=0.0, op0=ALU.mult, op1=ALU.add
-            )
-            t_of[k], neg_sum_of[k] = t_sb, neg_sum
+            t_of[k], row_sum_of[k] = t_sb, row_sum
+            if k % 2 == 0:
+                neg_sum = small.tile([P, 1], F32, tag="neg_sum")
+                nc.gpsimd.tensor_scalar(
+                    out=neg_sum[:], in0=row_sum[:], scalar1=-1.0, scalar2=0.0, op0=ALU.mult, op1=ALU.add
+                )
+                neg_sum_of[k] = neg_sum
 
         def minus_sum_probs(k):
             q, j = divmod(k, PAIR)
             m_sb = work.tile([P, CLASSES], F32, tag="m")
-            nc.scalar.activation(out=m_sb[:], in_=inputs[q]["probs"][:, j, :], func=ACT.Copy, scale=neg_sum_of[k][:])
+            if k % 2 == 0:
+                nc.scalar.activation(
+                    out=m_sb[:], in_=inputs[q]["probs"][:, j, :], func=ACT.Copy, scale=neg_sum_of[k][:]
+                )
+            else:
+                nc.vector.tensor_scalar(
+                    out=m_sb[:],
+                    in0=inputs[q]["probs"][:, j, :],
+                    scalar1=row_sum_of[k][:],
+                    scalar2=-1.0,
+                    op0=ALU.mult,
+                    op1=ALU.mult,
+                )
             m_of[k] = m_sb
 
         def x_sum_of_squares(k):
@@ -209,7 +234,7 @@ def tile_rbf_softmax_layer_t_v_kernel(tc, x, kernel, rbf, probs, grad_out, out):
                     out=r_of[q][:, g, t0 + h, :],
                     in_=rbf_turned_of[q, g, t0][:, h, :],
                     func=ACT.Copy,
-                    scale=rk10[g][:, t0 + h : t0 + h + 1],
+                    scale=rk10[:, g, t0 + h : t0 + h + 1],
                 )
 
         def turn_dl(k, g):
@@ -306,7 +331,7 @@ def tile_rbf_softmax_layer_t_v_kernel(tc, x, kernel, rbf, probs, grad_out, out):
                 op0=ALU.mult,
                 op1=ALU.add,
             )
-            nc.gpsimd.dma_start(out=out_pairs[q][:, j, :], in_=out_of[k][:])
+            nc.sync.dma_start(out=out_pairs[q][:, j, :], in_=out_of[k][:])
 
         def if_tile(stage, k, *more):
             if 0 <= k < TILES:
@@ -316,28 +341,44 @@ def tile_rbf_softmax_layer_t_v_kernel(tc, x, kernel, rbf, probs, grad_out, out):
             if 0 <= s < TILES:
                 stage(s // PAIR, s % PAIR, t0)
 
-        load_pair(0)
-        load_x(0)
-        load_pair(1)
-        for s in range(TILES + 5):
+        def step(s):
             if s % PAIR == 0 and s // PAIR + 1 < PAIRS:
                 load_x(s // PAIR + 1)
             if s % PAIR == 0 and s // PAIR + 2 < PAIRS:
                 load_pair(s // PAIR + 2)
-            if_tile(minus_sum_probs, s - 1)
+            if_tile(leave_psum, s - 4)
             if_tile(scale_dk, s - 3, 0)
             if_tile(scale_dk, s - 3, 1)
+            if_tile(turn_dl, s - 2, 0)
+            if_tile(turn_dl, s - 2, 1)
             if_step(scale_rbf, s - 1, 0)
             if_step(scale_rbf, s - 1, 2)
-            if_tile(pull_factor, s - 5)
-            if_tile(x_reciprocal_length, s - 3)
+            if_tile(dot_with_x, s - 5)
             if_tile(quantise_and_multiply, s - 3)
-            if_tile(turn_dl, s - 1, 0)
-            if_tile(turn_dl, s - 1, 1)
             if_step(turn_rbf, s, 0)
             if_step(turn_rbf, s, 2)
-            if_tile(project_and_store, s - 5)
+            if_tile(pull_factor, s - 5)
             if_tile(x_sum_of_squares, s - 2)
-            if_tile(front, s)
-            if_tile(leave_psum, s - 3)
-            if_tile(dot_with_x, s - 4)
+            if_tile(x_reciprocal_length, s - 3)
+            if_tile(front, s + 1)
+            if_tile(minus_sum_probs, s - 1)
+            if_tile(project_and_store, s - 5)
+
+        load_pair(0)
+        load_pair(1)
+        load_x(0)
+        for i in range(D_TILES // 2):
+            turn_kernel(i)
+        kernel_sums_of_squares(0)
+        for i in range(D_TILES // 2, D_TILES):
+            turn_kernel(i)
+        front(0)
+        step(0)
+        kernel_sums_of_squares(1)
+        kernel_table_rsqrt()
+        quantise_kernel(0)
+        kernel_newton_step()
+        step(1)
+        quantise_kernel(1)
+        for s in range(2, TILES + 5):
+            step(s)

@@ -71,7 +71,10 @@ def tile_rbf_softmax_layer_t_v_kernel(tc, x, kernel, rbf, probs, grad_out, out):
         k_grouped = keep.tile([P, PASSES, FEATURES, PACK], BF16, align_bytes=64)
         k_codes = keep.tile([P, PASSES, FEATURES], U32, align_bytes=64)
         k_scales = keep.tile([P, PASSES, FEATURES], U8, align_bytes=64)
-        k_partial = [keep.tile([P, 2, PACK], F32, name="k_partial%d" % g) for g in range(PASSES)]
+        k_partial = {}
+        for g in range(PASSES):
+            for half in range(2):
+                k_partial[g, half] = keep.tile([P, PACK], F32, name="k_partial%d%d" % (g, half))
         rk10 = keep.tile([P, PASSES, PACK], F32)
         k_a = keep.tile([P, PASSES, PACK], F32)
         k_y = keep.tile([P, PASSES, PACK], F32)
@@ -89,31 +92,24 @@ def tile_rbf_softmax_layer_t_v_kernel(tc, x, kernel, rbf, probs, grad_out, out):
             else:
                 nc.scalar.copy(out=grouped_view, in_=turned_view)
 
-        def kernel_sums_of_squares(half):
+        def kernel_sums_of_squares(g, half, engine):
             d0 = half * (FEATURES // 2)
             for t in range(PACK):
-                squares_s = work.tile([P, FEATURES // 2], BF16, tag="unread_s")
-                nc.scalar.activation(
-                    out=squares_s[:],
-                    in_=k_grouped[:, 0, d0 : d0 + FEATURES // 2, t],
-                    func=ACT.Square,
-                    accum_out=k_partial[0][:, half, t : t + 1],
-                )
-                squares_v = work.tile([P, FEATURES // 2], BF16, tag="unread_v")
-                nc.vector.scalar_tensor_tensor(
-                    out=squares_v[:],
-                    in0=k_grouped[:, 1, d0 : d0 + FEATURES // 2, t],
-                    scalar=1.0,
-                    in1=k_grouped[:, 1, d0 : d0 + FEATURES // 2, t],
-                    op0=ALU.mult,
-                    op1=ALU.mult,
-                    accum_out=k_partial[1][:, half, t : t + 1],
-                )
+                column = k_grouped[:, g, d0 : d0 + FEATURES // 2, t]
+                total = k_partial[g, half][:, t : t + 1]
+                if engine == "scalar":
+                    squares_s = work.tile([P, FEATURES // 2], BF16, tag="unread_s")
+                    nc.scalar.activation(out=squares_s[:], in_=column, func=ACT.Square, accum_out=total)
+                else:
+                    squares_v = work.tile([P, FEATURES // 2], BF16, tag="unread_v")
+                    nc.vector.scalar_tensor_tensor(
+                        out=squares_v[:], in0=column, scalar=1.0, in1=column, op0=ALU.mult, op1=ALU.mult, accum_out=total
+                    )
 
         def kernel_table_rsqrt():
             for g in range(PASSES):
                 nc.vector.tensor_tensor(
-                    out=k_a[:, g, :], in0=k_partial[g][:, 0, :], in1=k_partial[g][:, 1, :], op=ALU.add
+                    out=k_a[:, g, :], in0=k_partial[g, 0][:], in1=k_partial[g, 1][:], op=ALU.add
                 )
             nc.vector.tensor_scalar_max(out=k_a[:], in0=k_a[:], scalar1=EPS)
             inv_a = keep.tile([P, PASSES, PACK], F32)
@@ -145,7 +141,7 @@ def tile_rbf_softmax_layer_t_v_kernel(tc, x, kernel, rbf, probs, grad_out, out):
 
         inputs, t_of, m_of, r_of, dl_of, dk_of, de_of, out_of = {}, {}, {}, {}, {}, {}, {}, {}
         xx_floor_of, inv_xx_of, rx_of, ux_of, pull_of = {}, {}, {}, {}, {}
-        x_of, row_sum_of, neg_sum_of, rbf_turned_of = {}, {}, {}, {}
+        x_of, row_sum_of, rbf_turned_of = {}, {}, {}
 
         def load_pair(q):
             probs_sb = loads.tile([P, PAIR, CLASSES], F32, tag="probs")
@@ -175,29 +171,18 @@ def tile_rbf_softmax_layer_t_v_kernel(tc, x, kernel, rbf, probs, grad_out, out):
                 accum_out=row_sum[:],
             )
             t_of[k], row_sum_of[k] = t_sb, row_sum
-            if k % 2 == 0:
-                neg_sum = small.tile([P, 1], F32, tag="neg_sum")
-                nc.gpsimd.tensor_scalar(
-                    out=neg_sum[:], in0=row_sum[:], scalar1=-1.0, scalar2=0.0, op0=ALU.mult, op1=ALU.add
-                )
-                neg_sum_of[k] = neg_sum
 
         def minus_sum_probs(k):
             q, j = divmod(k, PAIR)
-            m_sb = work.tile([P, CLASSES], F32, tag="m")
-            if k % 2 == 0:
-                nc.scalar.activation(
-                    out=m_sb[:], in_=inputs[q]["probs"][:, j, :], func=ACT.Copy, scale=neg_sum_of[k][:]
-                )
-            else:
-                nc.vector.tensor_scalar(
-                    out=m_sb[:],
-                    in0=inputs[q]["probs"][:, j, :],
-                    scalar1=row_sum_of[k][:],
-                    scalar2=-1.0,
-                    op0=ALU.mult,
-                    op1=ALU.mult,
-                )
+            m_sb = work.tile([P, CLASSES], F32, tag="m", bufs=4)
+            nc.gpsimd.tensor_scalar(
+                out=m_sb[:],
+                in0=inputs[q]["probs"][:, j, :],
+                scalar1=row_sum_of[k][:],
+                scalar2=-1.0,
+                op0=ALU.mult,
+                op1=ALU.mult,
+            )
             m_of[k] = m_sb
 
         def x_sum_of_squares(k):
@@ -342,10 +327,10 @@ def tile_rbf_softmax_layer_t_v_kernel(tc, x, kernel, rbf, probs, grad_out, out):
                 stage(s // PAIR, s % PAIR, t0)
 
         def step(s):
-            if s % PAIR == 0 and s // PAIR + 1 < PAIRS:
-                load_x(s // PAIR + 1)
             if s % PAIR == 0 and s // PAIR + 2 < PAIRS:
                 load_pair(s // PAIR + 2)
+            if s % PAIR == 0 and s // PAIR + 1 < PAIRS:
+                load_x(s // PAIR + 1)
             if_tile(leave_psum, s - 4)
             if_tile(scale_dk, s - 3, 0)
             if_tile(scale_dk, s - 3, 1)
@@ -361,7 +346,7 @@ def tile_rbf_softmax_layer_t_v_kernel(tc, x, kernel, rbf, probs, grad_out, out):
             if_tile(x_sum_of_squares, s - 2)
             if_tile(x_reciprocal_length, s - 3)
             if_tile(front, s + 1)
-            if_tile(minus_sum_probs, s - 1)
+            if_tile(minus_sum_probs, s)
             if_tile(project_and_store, s - 5)
 
         load_pair(0)
@@ -369,16 +354,17 @@ def tile_rbf_softmax_layer_t_v_kernel(tc, x, kernel, rbf, probs, grad_out, out):
         load_x(0)
         for i in range(D_TILES // 2):
             turn_kernel(i)
-        kernel_sums_of_squares(0)
+        kernel_sums_of_squares(0, 0, "scalar")
+        kernel_sums_of_squares(1, 0, "vector")
         for i in range(D_TILES // 2, D_TILES):
             turn_kernel(i)
         front(0)
+        kernel_sums_of_squares(0, 1, "scalar")
+        kernel_sums_of_squares(1, 1, "scalar")
         step(0)
-        kernel_sums_of_squares(1)
-        kernel_table_rsqrt()
         quantise_kernel(0)
-        kernel_newton_step()
-        step(1)
         quantise_kernel(1)
-        for s in range(2, TILES + 5):
+        kernel_table_rsqrt()
+        kernel_newton_step()
+        for s in range(1, TILES + 5):
             step(s)

@@ -49,8 +49,8 @@ def tile_rbf_softmax_layer_t_v_kernel(tc, x, kernel, rbf, probs, grad_out, out):
         work = stack.enter_context(tc.tile_pool(name="work", bufs=3))
         small = stack.enter_context(tc.tile_pool(name="small", bufs=8))
         psum_dl = stack.enter_context(tc.psum_pool(name="psum_dl", bufs=2))
-        psum_rbf = stack.enter_context(tc.psum_pool(name="psum_rbf", bufs=2))
-        psum_de = stack.enter_context(tc.psum_pool(name="psum_de", bufs=4))
+        psum_rbf = stack.enter_context(tc.psum_pool(name="psum_rbf", bufs=4))
+        psum_de = stack.enter_context(tc.psum_pool(name="psum_de", bufs=2))
         stack.enter_context(tc.manual_schedule())
 
         ident_f32 = keep.tile([P, P], F32)
@@ -76,11 +76,9 @@ def tile_rbf_softmax_layer_t_v_kernel(tc, x, kernel, rbf, probs, grad_out, out):
             for half in range(2):
                 k_partial[g, half] = keep.tile([P, PACK], F32, name="k_partial%d%d" % (g, half))
         rk10 = keep.tile([P, PASSES, PACK], F32)
-        k_a = keep.tile([P, PASSES, PACK], F32)
-        k_y = keep.tile([P, PASSES, PACK], F32)
 
         def turn_kernel(i):
-            k_turned = psum_de.tile([P, PASSES, PACK, P], BF16, tag="de")
+            k_turned = psum_rbf.tile([P, PASSES, PACK, P], BF16, tag="rbf_turned")
             for g in range(PASSES):
                 for t in range(PACK):
                     c0 = g * K_PASS + t * P
@@ -106,7 +104,8 @@ def tile_rbf_softmax_layer_t_v_kernel(tc, x, kernel, rbf, probs, grad_out, out):
                         out=squares_v[:], in0=column, scalar=1.0, in1=column, op0=ALU.mult, op1=ALU.mult, accum_out=total
                     )
 
-        def kernel_table_rsqrt():
+        def kernel_reciprocal_lengths():
+            k_a = keep.tile([P, PASSES, PACK], F32)
             for g in range(PASSES):
                 nc.vector.tensor_tensor(
                     out=k_a[:, g, :], in0=k_partial[g, 0][:], in1=k_partial[g, 1][:], op=ALU.add
@@ -114,23 +113,7 @@ def tile_rbf_softmax_layer_t_v_kernel(tc, x, kernel, rbf, probs, grad_out, out):
             nc.vector.tensor_scalar_max(out=k_a[:], in0=k_a[:], scalar1=EPS)
             inv_a = keep.tile([P, PASSES, PACK], F32)
             nc.vector.reciprocal(out=inv_a[:], in_=k_a[:])
-            nc.scalar.activation(out=k_y[:], in_=inv_a[:], func=ACT.Sqrt)
-
-        def kernel_newton_step():
-            yy = keep.tile([P, PASSES, PACK], F32)
-            nc.vector.tensor_tensor(out=yy[:], in0=k_y[:], in1=k_y[:], op=ALU.mult)
-            ayy = keep.tile([P, PASSES, PACK], F32)
-            nc.vector.tensor_tensor(out=ayy[:], in0=yy[:], in1=k_a[:], op=ALU.mult)
-            factor = keep.tile([P, PASSES, PACK], F32)
-            nc.vector.tensor_scalar(
-                out=factor[:],
-                in0=ayy[:],
-                scalar1=-0.5 * LOGIT_SLOPE,
-                scalar2=1.5 * LOGIT_SLOPE,
-                op0=ALU.mult,
-                op1=ALU.add,
-            )
-            nc.vector.tensor_tensor(out=rk10[:], in0=k_y[:], in1=factor[:], op=ALU.mult)
+            nc.scalar.activation(out=rk10[:], in_=inv_a[:], func=ACT.Sqrt, scale=LOGIT_SLOPE * LOGIT_SLOPE)
 
         def quantise_kernel(g):
             nc.vector.quantize_mx(
@@ -364,7 +347,6 @@ def tile_rbf_softmax_layer_t_v_kernel(tc, x, kernel, rbf, probs, grad_out, out):
         step(0)
         quantise_kernel(0)
         quantise_kernel(1)
-        kernel_table_rsqrt()
-        kernel_newton_step()
+        kernel_reciprocal_lengths()
         for s in range(1, TILES + 5):
             step(s)

@@ -123,7 +123,7 @@ def tile_rbf_softmax_layer_t_v_kernel(tc, x, kernel, rbf, probs, grad_out, out):
             )
 
         inputs, t_of, m_of, r_of, dl_of, dk_of, de_of, out_of = {}, {}, {}, {}, {}, {}, {}, {}
-        xx_floor_of, inv_xx_of, rx_of, ux_of, pull_of = {}, {}, {}, {}, {}
+        xx_floor_of, inv_xx_of, rx_of, pull_of = {}, {}, {}, {}
         x_of, row_sum_of, rbf_turned_of = {}, {}, {}
 
         def load_pair(q):
@@ -174,14 +174,14 @@ def tile_rbf_softmax_layer_t_v_kernel(tc, x, kernel, rbf, probs, grad_out, out):
             xx = small.tile([P, 1], F32, tag="xx")
             nc.scalar.activation(out=squares[:], in_=x_of[q][:, j, :], func=ACT.Square, accum_out=xx[:])
             xx_floor = small.tile([P, 1], F32, tag="xx_floor")
-            nc.gpsimd.tensor_scalar_max(out=xx_floor[:], in0=xx[:], scalar1=EPS)
+            nc.gpsimd.tensor_scalar(out=xx_floor[:], in0=xx[:], scalar1=EPS, scalar2=-1.0, op0=ALU.max, op1=ALU.mult)
             xx_floor_of[k] = xx_floor
 
         def x_reciprocal_length(k):
             inv_xx = small.tile([P, 1], F32, tag="inv_xx")
             nc.vector.reciprocal(out=inv_xx[:], in_=xx_floor_of[k][:])
             rx = small.tile([P, 1], F32, tag="rx")
-            nc.scalar.activation(out=rx[:], in_=inv_xx[:], func=ACT.Sqrt)
+            nc.scalar.activation(out=rx[:], in_=inv_xx[:], func=ACT.Sqrt, scale=-1.0)
             inv_xx_of[k], rx_of[k] = inv_xx, rx
 
         def turn_rbf(q, g, t0):
@@ -232,9 +232,9 @@ def tile_rbf_softmax_layer_t_v_kernel(tc, x, kernel, rbf, probs, grad_out, out):
             if g == 0:
                 dk_of[k] = work.tile([P, PASSES, P, PACK], BF16, tag="dk_grouped", align_bytes=64, name="dk_grouped")
             nc.vector.tensor_tensor(
-                out=dk_of[k][:, g, :, :],
-                in0=dl_of[k, g][:].rearrange("p t b -> p b t"),
-                in1=r_of[q][:, g, :, j * P : (j + 1) * P].rearrange("p t b -> p b t"),
+                out=dk_of[k][:, g, :, :].rearrange("p (c i) t -> p c t i", i=4),
+                in0=dl_of[k, g][:].rearrange("p t (c i) -> p c t i", i=4),
+                in1=r_of[q][:, g, :, j * P : (j + 1) * P].rearrange("p t (c i) -> p c t i", i=4),
                 op=ALU.mult,
             )
 
@@ -270,22 +270,15 @@ def tile_rbf_softmax_layer_t_v_kernel(tc, x, kernel, rbf, probs, grad_out, out):
         def dot_with_x(k):
             q, j = divmod(k, PAIR)
             products = work.tile([P, FEATURES], BF16, tag="unread_v")
-            ux = small.tile([P, 1], F32, tag="ux")
+            pull = small.tile([P, 1], F32, tag="pull")
             nc.vector.scalar_tensor_tensor(
                 out=products[:],
                 in0=out_of[k][:],
-                scalar=1.0,
+                scalar=inv_xx_of[k][:],
                 in1=x_of[q][:, j, :],
                 op0=ALU.mult,
                 op1=ALU.mult,
-                accum_out=ux[:],
-            )
-            ux_of[k] = ux
-
-        def pull_factor(k):
-            pull = small.tile([P, 1], F32, tag="pull")
-            nc.vector.tensor_scalar(
-                out=pull[:], in0=ux_of[k][:], scalar1=inv_xx_of[k][:], scalar2=-1.0, op0=ALU.mult, op1=ALU.mult
+                accum_out=pull[:],
             )
             pull_of[k] = pull
 
@@ -325,7 +318,6 @@ def tile_rbf_softmax_layer_t_v_kernel(tc, x, kernel, rbf, probs, grad_out, out):
             if_tile(quantise_and_multiply, s - 3)
             if_step(turn_rbf, s, 0)
             if_step(turn_rbf, s, 2)
-            if_tile(pull_factor, s - 5)
             if_tile(x_sum_of_squares, s - 2)
             if_tile(x_reciprocal_length, s - 3)
             if_tile(front, s + 1)

@@ -307,6 +307,7 @@ def tile_rbf_softmax_layer_t_v_kernel(tc, x, kernel, rbf, probs, grad_out, out):
                 load_pair(s // PAIR + 2)
             if s % PAIR == 0 and s // PAIR + 1 < PAIRS:
                 load_x(s // PAIR + 1)
+            if_tile(minus_sum_probs, s)
             if_tile(leave_psum, s - 4)
             if_tile(scale_dk, s - 3, 0)
             if_tile(scale_dk, s - 3, 1)
@@ -321,7 +322,6 @@ def tile_rbf_softmax_layer_t_v_kernel(tc, x, kernel, rbf, probs, grad_out, out):
             if_tile(x_sum_of_squares, s - 2)
             if_tile(x_reciprocal_length, s - 3)
             if_tile(front, s + 1)
-            if_tile(minus_sum_probs, s)
             if_tile(project_and_store, s - 5)
 
         load_pair(0)

@@ -232,9 +232,9 @@ def tile_rbf_softmax_layer_t_v_kernel(tc, x, kernel, rbf, probs, grad_out, out):
             if g == 0:
                 dk_of[k] = work.tile([P, PASSES, P, PACK], BF16, tag="dk_grouped", align_bytes=64, name="dk_grouped")
             nc.vector.tensor_tensor(
-                out=dk_of[k][:, g, :, :].rearrange("p (c i) t -> p c t i", i=4),
-                in0=dl_of[k, g][:].rearrange("p t (c i) -> p c t i", i=4),
-                in1=r_of[q][:, g, :, j * P : (j + 1) * P].rearrange("p t (c i) -> p c t i", i=4),
+                out=dk_of[k][:, g, :, :].rearrange("p (c i) t -> p c t i", i=8),
+                in0=dl_of[k, g][:].rearrange("p t (c i) -> p c t i", i=8),
+                in1=r_of[q][:, g, :, j * P : (j + 1) * P].rearrange("p t (c i) -> p c t i", i=8),
                 op=ALU.mult,
             )
 

@@ -284,15 +284,19 @@ def tile_rbf_softmax_layer_t_v_kernel(tc, x, kernel, rbf, probs, grad_out, out):
 
         def project_and_store(k):
             q, j = divmod(k, PAIR)
-            nc.vector.scalar_tensor_tensor(
-                out=out_of[k][:],
-                in0=x_of[q][:, j, :],
-                scalar=pull_of[k][:],
-                in1=out_of[k][:],
-                op0=ALU.mult,
-                op1=ALU.add,
-            )
-            nc.sync.dma_start(out=out_pairs[q][:, j, :], in_=out_of[k][:])
+            pieces = N_HALVES if k == TILES - 1 else 1
+            width = FEATURES // pieces
+            for n in range(pieces):
+                cols = slice(n * width, (n + 1) * width)
+                nc.vector.scalar_tensor_tensor(
+                    out=out_of[k][:, cols],
+                    in0=x_of[q][:, j, cols],
+                    scalar=pull_of[k][:],
+                    in1=out_of[k][:, cols],
+                    op0=ALU.mult,
+                    op1=ALU.add,
+                )
+                nc.sync.dma_start(out=out_pairs[q][:, j, cols], in_=out_of[k][:, cols])
 
         def if_tile(stage, k, *more):
             if 0 <= k < TILES:

@@ -158,14 +158,11 @@ def tile_rbf_softmax_layer_t_v_kernel(tc, x, kernel, rbf, probs, grad_out, out):
         def minus_sum_probs(k):
             q, j = divmod(k, PAIR)
             m_sb = work.tile([P, CLASSES], F32, tag="m", bufs=4)
+            minus_sum = small.tile([P, 1], F32, tag="minus_sum")
             nc.gpsimd.tensor_scalar(
-                out=m_sb[:],
-                in0=inputs[q]["probs"][:, j, :],
-                scalar1=row_sum_of[k][:],
-                scalar2=-1.0,
-                op0=ALU.mult,
-                op1=ALU.mult,
+                out=minus_sum[:], in0=row_sum_of[k][:], scalar1=-1.0, scalar2=1.0, op0=ALU.mult, op1=ALU.mult
             )
+            nc.scalar.activation(out=m_sb[:], in_=inputs[q]["probs"][:, j, :], func=ACT.Copy, scale=minus_sum[:])
             m_of[k] = m_sb
 
         def x_sum_of_squares(k):
@@ -311,7 +308,6 @@ def tile_rbf_softmax_layer_t_v_kernel(tc, x, kernel, rbf, probs, grad_out, out):
                 load_pair(s // PAIR + 2)
             if s % PAIR == 0 and s // PAIR + 1 < PAIRS:
                 load_x(s // PAIR + 1)
-            if_tile(minus_sum_probs, s)
             if_tile(leave_psum, s - 4)
             if_tile(scale_dk, s - 3, 0)
             if_tile(scale_dk, s - 3, 1)
@@ -323,6 +319,7 @@ def tile_rbf_softmax_layer_t_v_kernel(tc, x, kernel, rbf, probs, grad_out, out):
             if_tile(quantise_and_multiply, s - 3)
             if_step(turn_rbf, s, 0)
             if_step(turn_rbf, s, 2)
+            if_tile(minus_sum_probs, s)
             if_tile(x_sum_of_squares, s - 2)
             if_tile(x_reciprocal_length, s - 3)
             if_tile(front, s + 1)

@@ -123,7 +123,7 @@ def tile_rbf_softmax_layer_t_v_kernel(tc, x, kernel, rbf, probs, grad_out, out):
             )
 
         inputs, t_of, m_of, r_of, dl_of, dk_of, de_of, out_of = {}, {}, {}, {}, {}, {}, {}, {}
-        xx_floor_of, inv_xx_of, rx_of, pull_of = {}, {}, {}, {}
+        xx_of, xx_floor_of, inv_xx_of, rx_of, pull_of, minus_sum_of = {}, {}, {}, {}, {}, {}
         x_of, row_sum_of, rbf_turned_of = {}, {}, {}
 
         def load_pair(q):
@@ -157,29 +157,48 @@ def tile_rbf_softmax_layer_t_v_kernel(tc, x, kernel, rbf, probs, grad_out, out):
 
         def minus_sum_probs(k):
             q, j = divmod(k, PAIR)
-            m_sb = work.tile([P, CLASSES], F32, tag="m", bufs=4)
-            minus_sum = small.tile([P, 1], F32, tag="minus_sum")
+            m_lo = work.tile([P, K_PASS], F32, tag="m_lo", bufs=4)
+            m_hi = work.tile([P, K_PASS], F32, tag="m_hi", bufs=4)
             nc.gpsimd.tensor_scalar(
-                out=minus_sum[:], in0=row_sum_of[k][:], scalar1=-1.0, scalar2=1.0, op0=ALU.mult, op1=ALU.mult
+                out=m_hi[:],
+                in0=inputs[q]["probs"][:, j, K_PASS:CLASSES],
+                scalar1=row_sum_of[k][:],
+                scalar2=-1.0,
+                op0=ALU.mult,
+                op1=ALU.mult,
             )
-            nc.scalar.activation(out=m_sb[:], in_=inputs[q]["probs"][:, j, :], func=ACT.Copy, scale=minus_sum[:])
-            m_of[k] = m_sb
+            nc.scalar.activation(
+                out=m_lo[:], in_=inputs[q]["probs"][:, j, 0:K_PASS], func=ACT.Copy, scale=minus_sum_of[k][:]
+            )
+            m_of[k] = [m_lo, m_hi]
+
+        def minus_row_sum(k):
+            minus_sum = small.tile([P, 1], F32, tag="minus_sum")
+            nc.scalar.mul(out=minus_sum[:], in_=row_sum_of[k][:], mul=-1.0)
+            minus_sum_of[k] = minus_sum
 
         def x_sum_of_squares(k):
             q, j = divmod(k, PAIR)
+            if j == 0:
+                xx_of[q] = small.tile([P, PAIR], F32, tag="xx", name="xx")
             squares = work.tile([P, FEATURES], BF16, tag="unread_s")
-            xx = small.tile([P, 1], F32, tag="xx")
-            nc.scalar.activation(out=squares[:], in_=x_of[q][:, j, :], func=ACT.Square, accum_out=xx[:])
-            xx_floor = small.tile([P, 1], F32, tag="xx_floor")
-            nc.gpsimd.tensor_scalar(out=xx_floor[:], in0=xx[:], scalar1=EPS, scalar2=-1.0, op0=ALU.max, op1=ALU.mult)
-            xx_floor_of[k] = xx_floor
+            nc.scalar.activation(
+                out=squares[:], in_=x_of[q][:, j, :], func=ACT.Square, accum_out=xx_of[q][:, j : j + 1]
+            )
 
-        def x_reciprocal_length(k):
-            inv_xx = small.tile([P, 1], F32, tag="inv_xx")
-            nc.vector.reciprocal(out=inv_xx[:], in_=xx_floor_of[k][:])
-            rx = small.tile([P, 1], F32, tag="rx")
+        def x_floor(q):
+            xx_floor = small.tile([P, PAIR], F32, tag="xx_floor")
+            nc.vector.tensor_scalar(
+                out=xx_floor[:], in0=xx_of[q][:], scalar1=EPS, scalar2=-1.0, op0=ALU.max, op1=ALU.mult
+            )
+            xx_floor_of[q] = xx_floor
+
+        def x_reciprocal_lengths(q):
+            inv_xx = small.tile([P, PAIR], F32, tag="inv_xx")
+            nc.vector.reciprocal(out=inv_xx[:], in_=xx_floor_of[q][:])
+            rx = small.tile([P, PAIR], F32, tag="rx")
             nc.scalar.activation(out=rx[:], in_=inv_xx[:], func=ACT.Sqrt, scale=-1.0)
-            inv_xx_of[k], rx_of[k] = inv_xx, rx
+            inv_xx_of[q], rx_of[q] = inv_xx, rx
 
         def turn_rbf(q, g, t0):
             rbf_turned = psum_rbf.tile([P, 2, PAIR * P], F32, tag="rbf_turned")
@@ -216,7 +235,7 @@ def tile_rbf_softmax_layer_t_v_kernel(tc, x, kernel, rbf, probs, grad_out, out):
                 )
                 nc.tensor.matmul(
                     out=dl_turned[:, t, :],
-                    lhsT=m_of[k][:, c0 : c0 + P],
+                    lhsT=m_of[k][g][:, t * P : (t + 1) * P],
                     rhs=ident_f32[:],
                     is_transpose=True,
                     start=False,
@@ -257,10 +276,11 @@ def tile_rbf_softmax_layer_t_v_kernel(tc, x, kernel, rbf, probs, grad_out, out):
                     )
 
         def leave_psum(k):
+            q, j = divmod(k, PAIR)
             out_sb = work.tile([P, FEATURES], F32, tag="out", bufs=4)
             for n in range(N_HALVES):
                 nc.scalar.activation(
-                    out=out_sb[:, n * N_COLS : (n + 1) * N_COLS], in_=de_of[k][n][:], func=ACT.Copy, scale=rx_of[k][:]
+                    out=out_sb[:, n * N_COLS : (n + 1) * N_COLS], in_=de_of[k][n][:], func=ACT.Copy, scale=rx_of[q][:, j : j + 1]
                 )
             out_of[k] = out_sb
 
@@ -271,7 +291,7 @@ def tile_rbf_softmax_layer_t_v_kernel(tc, x, kernel, rbf, probs, grad_out, out):
             nc.vector.scalar_tensor_tensor(
                 out=products[:],
                 in0=out_of[k][:],
-                scalar=inv_xx_of[k][:],
+                scalar=inv_xx_of[q][:, j : j + 1],
                 in1=x_of[q][:, j, :],
                 op0=ALU.mult,
                 op1=ALU.mult,
@@ -299,6 +319,10 @@ def tile_rbf_softmax_layer_t_v_kernel(tc, x, kernel, rbf, probs, grad_out, out):
             if 0 <= k < TILES:
                 stage(k, *more)
 
+        def if_pair(stage, k):
+            if k % PAIR == 0 and 0 <= k < TILES:
+                stage(k // PAIR)
+
         def if_step(stage, s, t0):
             if 0 <= s < TILES:
                 stage(s // PAIR, s % PAIR, t0)
@@ -309,20 +333,22 @@ def tile_rbf_softmax_layer_t_v_kernel(tc, x, kernel, rbf, probs, grad_out, out):
             if s % PAIR == 0 and s // PAIR + 1 < PAIRS:
                 load_x(s // PAIR + 1)
             if_tile(leave_psum, s - 4)
+            if_tile(minus_row_sum, s)
             if_tile(scale_dk, s - 3, 0)
             if_tile(scale_dk, s - 3, 1)
             if_tile(turn_dl, s - 2, 0)
             if_tile(turn_dl, s - 2, 1)
             if_step(scale_rbf, s - 1, 0)
             if_step(scale_rbf, s - 1, 2)
+            if_tile(minus_sum_probs, s)
             if_tile(dot_with_x, s - 5)
             if_tile(quantise_and_multiply, s - 3)
             if_step(turn_rbf, s, 0)
             if_step(turn_rbf, s, 2)
-            if_tile(minus_sum_probs, s)
-            if_tile(x_sum_of_squares, s - 2)
-            if_tile(x_reciprocal_length, s - 3)
+            if_tile(x_sum_of_squares, s - 1)
+            if_pair(x_floor, s - 3)
             if_tile(front, s + 1)
+            if_pair(x_reciprocal_lengths, s - 3)
             if_tile(project_and_store, s - 5)
 
         load_pair(0)

@@ -24,6 +24,7 @@ PAIRS = TOKENS // (PAIR * P)
 TILES = TOKENS // P
 D_TILES = FEATURES // P
 EPS = 1e-12
+VEC_EVAC = (0, 2, 4)
 LOGIT_SLOPE = 100.0 * 2.0 / 20.0
 
 FLOPS = 2 * TOKENS * FEATURES * CLASSES
@@ -62,20 +63,24 @@ def tile_rbf_softmax_layer_t_v_kernel(tc, x, kernel, rbf, probs, grad_out, out):
         warm = keep.tile([P, 1], F32)
         nc.scalar.activation(out=warm[:], in_=one[:], func=ACT.Sqrt)
 
+        zeros = keep.tile([P, N_COLS], BF16)
+        nc.vector.memset(zeros[:], 0.0)
+
         k_rows = keep.tile([P, D_TILES, CLASSES], BF16)
-        for i in range(0, D_TILES, 2):
-            nc.sync.dma_start(
-                out=k_rows[:, i : i + 2, :],
-                in_=kernel[i * P : (i + 2) * P, :].rearrange("(i p) c -> p i c", p=P),
-            )
         k_grouped = keep.tile([P, PASSES, FEATURES, PACK], BF16, align_bytes=64)
         k_codes = keep.tile([P, PASSES, FEATURES], U32, align_bytes=64)
         k_scales = keep.tile([P, PASSES, FEATURES], U8, align_bytes=64)
-        k_partial = {}
-        for g in range(PASSES):
-            for half in range(2):
-                k_partial[g, half] = keep.tile([P, PACK], F32, name="k_partial%d%d" % (g, half))
+        k_squares = keep.tile([P, PASSES, PACK], F32)
+        gram_banks = [psum_de.tile([P, PACK, P], F32, tag="de", name="gram%d" % n) for n in range(2)]
+        gram_banks += [psum_dl.tile([P, PACK, P], F32, tag="dl_turned", name="gram%d" % n) for n in range(2, 4)]
         rk10 = keep.tile([P, PASSES, PACK], F32)
+        k_floor = keep.tile([P, PASSES, PACK], F32)
+
+        def load_kernel(i, tiles):
+            nc.sync.dma_start(
+                out=k_rows[:, i : i + tiles, :],
+                in_=kernel[i * P : (i + tiles) * P, :].rearrange("(i p) c -> p i c", p=P),
+            )
 
         def turn_kernel(i):
             k_turned = psum_rbf.tile([P, PASSES, PACK, P], BF16, tag="rbf_turned")
@@ -85,35 +90,38 @@ def tile_rbf_softmax_layer_t_v_kernel(tc, x, kernel, rbf, probs, grad_out, out):
                     nc.tensor.transpose(k_turned[:, g, t, :], k_rows[:, i, c0 : c0 + P], ident_bf16[:])
             grouped_view = k_grouped[:, :, i * P : (i + 1) * P, :]
             turned_view = k_turned[:].rearrange("p g t r -> p g r t")
-            if i % 2 == 0:
+            if i in VEC_EVAC:
                 nc.vector.tensor_copy(out=grouped_view, in_=turned_view)
             else:
                 nc.scalar.copy(out=grouped_view, in_=turned_view)
 
-        def kernel_sums_of_squares(g, half, engine):
-            d0 = half * (FEATURES // 2)
+        def gram(g, t, i):
+            c0 = g * K_PASS + t * P
+            block = k_rows[:, i, c0 : c0 + P]
+            nc.tensor.matmul(
+                out=gram_banks[t][:, g, :], lhsT=block, rhs=block, start=(i == 0), stop=(i == D_TILES - 1)
+            )
+
+        def gram_diagonals(g):
             for t in range(PACK):
-                column = k_grouped[:, g, d0 : d0 + FEATURES // 2, t]
-                total = k_partial[g, half][:, t : t + 1]
-                if engine == "scalar":
-                    squares_s = work.tile([P, FEATURES // 2], BF16, tag="unread_s")
-                    nc.scalar.activation(out=squares_s[:], in_=column, func=ACT.Square, accum_out=total)
-                else:
-                    squares_v = work.tile([P, FEATURES // 2], BF16, tag="unread_v")
-                    nc.vector.scalar_tensor_tensor(
-                        out=squares_v[:], in0=column, scalar=1.0, in1=column, op0=ALU.mult, op1=ALU.mult, accum_out=total
-                    )
+                diagonal = work.tile([P, P], BF16, tag="unread_d")
+                nc.vector.scalar_tensor_tensor(
+                    out=diagonal[:],
+                    in0=gram_banks[t][:, g, :],
+                    scalar=1.0,
+                    in1=ident_f32[:],
+                    op0=ALU.mult,
+                    op1=ALU.mult,
+                    accum_out=k_squares[:, g, t : t + 1],
+                )
+
+        def kernel_floor():
+            nc.vector.tensor_scalar_max(out=k_floor[:], in0=k_squares[:], scalar1=EPS)
 
         def kernel_reciprocal_lengths():
-            k_a = keep.tile([P, PASSES, PACK], F32)
-            for g in range(PASSES):
-                nc.vector.tensor_tensor(
-                    out=k_a[:, g, :], in0=k_partial[g, 0][:], in1=k_partial[g, 1][:], op=ALU.add
-                )
-            nc.vector.tensor_scalar_max(out=k_a[:], in0=k_a[:], scalar1=EPS)
-            inv_a = keep.tile([P, PASSES, PACK], F32)
-            nc.vector.reciprocal(out=inv_a[:], in_=k_a[:])
-            nc.scalar.activation(out=rk10[:], in_=inv_a[:], func=ACT.Sqrt, scale=LOGIT_SLOPE * LOGIT_SLOPE)
+            inv = keep.tile([P, PASSES, PACK], F32)
+            nc.vector.reciprocal(out=inv[:], in_=k_floor[:])
+            nc.scalar.activation(out=rk10[:], in_=inv[:], func=ACT.Sqrt, scale=LOGIT_SLOPE * LOGIT_SLOPE)
 
         def quantise_kernel(g):
             nc.vector.quantize_mx(
@@ -122,18 +130,35 @@ def tile_rbf_softmax_layer_t_v_kernel(tc, x, kernel, rbf, probs, grad_out, out):
                 in_=k_grouped[:, g, :, :].rearrange("p d t -> p (d t)"),
             )
 
+        def warm_up():
+            nc.tensor.matmul(out=gram_banks[0][:].rearrange("p g c -> p (g c)"), lhsT=zeros[:, 0:P], rhs=zeros[:], start=True, stop=True)
+
+        def warm_up2():
+            bank = psum_rbf.tile([P, N_COLS], F32, tag="rbf_turned", name="warm_bank")
+            nc.tensor.matmul(out=bank[:], lhsT=zeros[:, 0:P], rhs=zeros[:], start=True, stop=True)
+
         inputs, t_of, m_of, r_of, dl_of, dk_of, de_of, out_of = {}, {}, {}, {}, {}, {}, {}, {}
         xx_of, xx_floor_of, inv_xx_of, rx_of, pull_of, minus_sum_of = {}, {}, {}, {}, {}, {}
         x_of, row_sum_of, rbf_turned_of = {}, {}, {}
 
+        def open_pair(q):
+            inputs[q] = {
+                "probs": loads.tile([P, PAIR, CLASSES], F32, tag="probs", name="probs"),
+                "grad": loads.tile([P, PAIR, CLASSES], BF16, tag="grad", name="grad"),
+                "rbf": loads.tile([P, PAIR, CLASSES], F32, tag="rbf", name="rbf"),
+            }
+
+        def load_front(q, j, tiles):
+            nc.sync.dma_start(out=inputs[q]["probs"][:, j : j + tiles, :], in_=probs_pairs[q][:, j : j + tiles, :])
+            nc.sync.dma_start(out=inputs[q]["grad"][:, j : j + tiles, :], in_=grad_pairs[q][:, j : j + tiles, :])
+
+        def load_rbf(q):
+            nc.sync.dma_start(out=inputs[q]["rbf"][:], in_=rbf_pairs[q])
+
         def load_pair(q):
-            probs_sb = loads.tile([P, PAIR, CLASSES], F32, tag="probs")
-            nc.sync.dma_start(out=probs_sb[:], in_=probs_pairs[q])
-            grad_sb = loads.tile([P, PAIR, CLASSES], BF16, tag="grad")
-            nc.sync.dma_start(out=grad_sb[:], in_=grad_pairs[q])
-            rbf_sb = loads.tile([P, PAIR, CLASSES], F32, tag="rbf")
-            nc.sync.dma_start(out=rbf_sb[:], in_=rbf_pairs[q])
-            inputs[q] = {"probs": probs_sb, "grad": grad_sb, "rbf": rbf_sb}
+            open_pair(q)
+            load_front(q, 0, PAIR)
+            load_rbf(q)
 
         def load_x(q):
             x_sb = loads.tile([P, PAIR, FEATURES], BF16, tag="x", bufs=5)
@@ -328,44 +353,83 @@ def tile_rbf_softmax_layer_t_v_kernel(tc, x, kernel, rbf, probs, grad_out, out):
                 stage(s // PAIR, s % PAIR, t0)
 
         def step(s):
-            if s % PAIR == 0 and s // PAIR + 2 < PAIRS:
-                load_pair(s // PAIR + 2)
             if s % PAIR == 0 and s // PAIR + 1 < PAIRS:
                 load_x(s // PAIR + 1)
+            if s % PAIR == 0 and s // PAIR + 2 < PAIRS:
+                load_pair(s // PAIR + 2)
             if_tile(leave_psum, s - 4)
-            if_tile(minus_row_sum, s)
+            if_tile(minus_row_sum, s - 1)
             if_tile(scale_dk, s - 3, 0)
             if_tile(scale_dk, s - 3, 1)
             if_tile(turn_dl, s - 2, 0)
             if_tile(turn_dl, s - 2, 1)
             if_step(scale_rbf, s - 1, 0)
             if_step(scale_rbf, s - 1, 2)
-            if_tile(minus_sum_probs, s)
+            if_tile(minus_sum_probs, s - 1)
             if_tile(dot_with_x, s - 5)
             if_tile(quantise_and_multiply, s - 3)
             if_step(turn_rbf, s, 0)
             if_step(turn_rbf, s, 2)
             if_tile(x_sum_of_squares, s - 1)
             if_pair(x_floor, s - 3)
-            if_tile(front, s + 1)
+            if_tile(front, s)
             if_pair(x_reciprocal_lengths, s - 3)
             if_tile(project_and_store, s - 5)
 
-        load_pair(0)
-        load_pair(1)
+        open_pair(0)
+        load_kernel(0, 1)
+        load_kernel(1, 1)
+        load_kernel(2, 2)
+        load_front(0, 0, 1)
+        load_kernel(4, 2)
+        load_kernel(6, 2)
+        load_front(0, 1, 1)
+        load_rbf(0)
         load_x(0)
-        for i in range(D_TILES // 2):
+        load_pair(1)
+        for n in range(4):
+            warm_up()
+        for i in range(D_TILES):
             turn_kernel(i)
-        kernel_sums_of_squares(0, 0, "scalar")
-        kernel_sums_of_squares(1, 0, "vector")
-        for i in range(D_TILES // 2, D_TILES):
-            turn_kernel(i)
-        front(0)
-        kernel_sums_of_squares(0, 1, "scalar")
-        kernel_sums_of_squares(1, 1, "scalar")
-        step(0)
+            for t in range(PACK):
+                gram(0, t, i)
+            if i == 5:
+                front(0)
+        for t in range(PACK):
+            for i in range(D_TILES):
+                gram(1, t, i)
+        turn_rbf(0, 0, 0)
+        turn_rbf(0, 0, 2)
+        turn_rbf(0, 1, 0)
+        turn_rbf(0, 1, 2)
+        front(1)
+        minus_row_sum(0)
+        minus_sum_probs(0)
+        minus_row_sum(1)
+        minus_sum_probs(1)
+        load_x(1)
+        load_pair(2)
+        gram_diagonals(0)
+        gram_diagonals(1)
+        kernel_floor()
+        x_sum_of_squares(0)
+        kernel_reciprocal_lengths()
+        turn_dl(0, 0)
+        turn_dl(0, 1)
+        scale_rbf(0, 0, 0)
+        scale_rbf(0, 0, 2)
+        scale_rbf(0, 1, 0)
+        scale_rbf(0, 1, 2)
         quantise_kernel(0)
         quantise_kernel(1)
-        kernel_reciprocal_lengths()
-        for s in range(1, TILES + 5):
+        warm_up2()
+        warm_up2()
+        warm_up2()
+        turn_rbf(1, 0, 0)
+        turn_rbf(1, 0, 2)
+        x_sum_of_squares(1)
+        load_x(2)
+        load_pair(3)
+        front(2)
+        for s in range(3, TILES + 5):
             step(s)

@@ -24,7 +24,6 @@ PAIRS = TOKENS // (PAIR * P)
 TILES = TOKENS // P
 D_TILES = FEATURES // P
 EPS = 1e-12
-VEC_EVAC = (0, 2, 4)
 LOGIT_SLOPE = 100.0 * 2.0 / 20.0
 
 FLOPS = 2 * TOKENS * FEATURES * CLASSES
@@ -63,7 +62,7 @@ def tile_rbf_softmax_layer_t_v_kernel(tc, x, kernel, rbf, probs, grad_out, out):
         warm = keep.tile([P, 1], F32)
         nc.scalar.activation(out=warm[:], in_=one[:], func=ACT.Sqrt)
 
-        zeros = keep.tile([P, N_COLS], BF16)
+        zeros = keep.tile([P, P], F32)
         nc.vector.memset(zeros[:], 0.0)
 
         k_rows = keep.tile([P, D_TILES, CLASSES], BF16)
@@ -88,12 +87,9 @@ def tile_rbf_softmax_layer_t_v_kernel(tc, x, kernel, rbf, probs, grad_out, out):
                 for t in range(PACK):
                     c0 = g * K_PASS + t * P
                     nc.tensor.transpose(k_turned[:, g, t, :], k_rows[:, i, c0 : c0 + P], ident_bf16[:])
-            grouped_view = k_grouped[:, :, i * P : (i + 1) * P, :]
-            turned_view = k_turned[:].rearrange("p g t r -> p g r t")
-            if i in VEC_EVAC:
-                nc.vector.tensor_copy(out=grouped_view, in_=turned_view)
-            else:
-                nc.scalar.copy(out=grouped_view, in_=turned_view)
+            nc.scalar.copy(
+                out=k_grouped[:, :, i * P : (i + 1) * P, :], in_=k_turned[:].rearrange("p g t r -> p g r t")
+            )
 
         def gram(g, t, i):
             c0 = g * K_PASS + t * P
@@ -130,12 +126,10 @@ def tile_rbf_softmax_layer_t_v_kernel(tc, x, kernel, rbf, probs, grad_out, out):
                 in_=k_grouped[:, g, :, :].rearrange("p d t -> p (d t)"),
             )
 
-        def warm_up():
-            nc.tensor.matmul(out=gram_banks[0][:].rearrange("p g c -> p (g c)"), lhsT=zeros[:, 0:P], rhs=zeros[:], start=True, stop=True)
-
-        def warm_up2():
-            bank = psum_rbf.tile([P, N_COLS], F32, tag="rbf_turned", name="warm_bank")
-            nc.tensor.matmul(out=bank[:], lhsT=zeros[:, 0:P], rhs=zeros[:], start=True, stop=True)
+        def warm_up(passes):
+            bank = psum_rbf.tile([P, P], F32, tag="rbf_turned", name="warm_bank")
+            for n in range(passes):
+                nc.tensor.matmul(out=bank[:], lhsT=zeros[:], rhs=zeros[:], start=True, stop=True)
 
         inputs, t_of, m_of, r_of, dl_of, dk_of, de_of, out_of = {}, {}, {}, {}, {}, {}, {}, {}
         xx_of, xx_floor_of, inv_xx_of, rx_of, pull_of, minus_sum_of = {}, {}, {}, {}, {}, {}
@@ -372,28 +366,29 @@ def tile_rbf_softmax_layer_t_v_kernel(tc, x, kernel, rbf, probs, grad_out, out):
             if_step(turn_rbf, s, 2)
             if_tile(x_sum_of_squares, s - 1)
             if_pair(x_floor, s - 3)
-            if_tile(front, s)
-            if_pair(x_reciprocal_lengths, s - 3)
             if_tile(project_and_store, s - 5)
+            if_pair(x_reciprocal_lengths, s - 3)
+            if_tile(front, s)
 
         open_pair(0)
+        open_pair(1)
         load_kernel(0, 1)
         load_kernel(1, 1)
         load_kernel(2, 2)
-        load_front(0, 0, 1)
         load_kernel(4, 2)
+        load_front(0, 0, 1)
         load_kernel(6, 2)
         load_front(0, 1, 1)
         load_rbf(0)
         load_x(0)
-        load_pair(1)
-        for n in range(4):
-            warm_up()
+        load_front(1, 0, 2)
+        load_rbf(1)
+        warm_up(6)
         for i in range(D_TILES):
             turn_kernel(i)
             for t in range(PACK):
                 gram(0, t, i)
-            if i == 5:
+            if i == 3:
                 front(0)
         for t in range(PACK):
             for i in range(D_TILES):
@@ -412,19 +407,18 @@ def tile_rbf_softmax_layer_t_v_kernel(tc, x, kernel, rbf, probs, grad_out, out):
         gram_diagonals(0)
         gram_diagonals(1)
         kernel_floor()
-        x_sum_of_squares(0)
         kernel_reciprocal_lengths()
+        warm_up(3)
         turn_dl(0, 0)
         turn_dl(0, 1)
         scale_rbf(0, 0, 0)
         scale_rbf(0, 0, 2)
         scale_rbf(0, 1, 0)
         scale_rbf(0, 1, 2)
+        x_sum_of_squares(0)
         quantise_kernel(0)
         quantise_kernel(1)
-        warm_up2()
-        warm_up2()
-        warm_up2()
+        warm_up(6)
         turn_rbf(1, 0, 0)
         turn_rbf(1, 0, 2)
         x_sum_of_squares(1)

@@ -87,9 +87,12 @@ def tile_rbf_softmax_layer_t_v_kernel(tc, x, kernel, rbf, probs, grad_out, out):
                 for t in range(PACK):
                     c0 = g * K_PASS + t * P
                     nc.tensor.transpose(k_turned[:, g, t, :], k_rows[:, i, c0 : c0 + P], ident_bf16[:])
-            nc.scalar.copy(
-                out=k_grouped[:, :, i * P : (i + 1) * P, :], in_=k_turned[:].rearrange("p g t r -> p g r t")
-            )
+            grouped_view = k_grouped[:, :, i * P : (i + 1) * P, :]
+            turned_view = k_turned[:].rearrange("p g t r -> p g r t")
+            if i in (0, 2, 4):
+                nc.vector.tensor_copy(out=grouped_view, in_=turned_view)
+            else:
+                nc.scalar.copy(out=grouped_view, in_=turned_view)
 
         def gram(g, t, i):
             c0 = g * K_PASS + t * P
@@ -388,7 +391,7 @@ def tile_rbf_softmax_layer_t_v_kernel(tc, x, kernel, rbf, probs, grad_out, out):
             turn_kernel(i)
             for t in range(PACK):
                 gram(0, t, i)
-            if i == 3:
+            if i == 5:
                 front(0)
         for t in range(PACK):
             for i in range(D_TILES):

@@ -59,6 +59,8 @@ def tile_rbf_softmax_layer_t_v_kernel(tc, x, kernel, rbf, probs, grad_out, out):
         make_identity(nc, ident_bf16[:])
         one = keep.tile([P, 1], F32)
         nc.vector.memset(one[:], 1.0)
+        minus_eps = keep.tile([P, 1], F32)
+        nc.vector.memset(minus_eps[:], -EPS)
         warm = keep.tile([P, 1], F32)
         nc.scalar.activation(out=warm[:], in_=one[:], func=ACT.Sqrt)
 
@@ -210,9 +212,9 @@ def tile_rbf_softmax_layer_t_v_kernel(tc, x, kernel, rbf, probs, grad_out, out):
 
         def x_floor(q):
             xx_floor = small.tile([P, PAIR], F32, tag="xx_floor")
-            nc.vector.tensor_scalar(
-                out=xx_floor[:], in0=xx_of[q][:], scalar1=EPS, scalar2=-1.0, op0=ALU.max, op1=ALU.mult
-            )
+            above = small.tile([P, PAIR], F32, tag="above")
+            nc.scalar.activation(out=above[:], in_=xx_of[q][:], func=ACT.Relu, bias=minus_eps[:])
+            nc.scalar.activation(out=xx_floor[:], in_=above[:], func=ACT.Identity, scale=-1.0, bias=minus_eps[:])
             xx_floor_of[q] = xx_floor
 
         def x_reciprocal_lengths(q):
@@ -365,12 +367,12 @@ def tile_rbf_softmax_layer_t_v_kernel(tc, x, kernel, rbf, probs, grad_out, out):
             if_tile(minus_sum_probs, s - 1)
             if_tile(dot_with_x, s - 5)
             if_tile(quantise_and_multiply, s - 3)
+            if_pair(x_reciprocal_lengths, s - 3)
             if_step(turn_rbf, s, 0)
             if_step(turn_rbf, s, 2)
             if_tile(x_sum_of_squares, s - 1)
-            if_pair(x_floor, s - 3)
+            if_pair(x_floor, s - 2)
             if_tile(project_and_store, s - 5)
-            if_pair(x_reciprocal_lengths, s - 3)
             if_tile(front, s)
 
         open_pair(0)
@@ -425,6 +427,7 @@ def tile_rbf_softmax_layer_t_v_kernel(tc, x, kernel, rbf, probs, grad_out, out):
         turn_rbf(1, 0, 0)
         turn_rbf(1, 0, 2)
         x_sum_of_squares(1)
+        x_floor(0)
         load_x(2)
         load_pair(3)
         front(2)

@@ -26,6 +26,7 @@ D_TILES = FEATURES // P
 EPS = 1e-12
 LOGIT_SLOPE = 100.0 * 2.0 / 20.0
 
+LEAD_FROM = 4
 FLOPS = 2 * TOKENS * FEATURES * CLASSES
 
 
@@ -357,14 +358,20 @@ def tile_rbf_softmax_layer_t_v_kernel(tc, x, kernel, rbf, probs, grad_out, out):
             if s % PAIR == 0 and s // PAIR + 2 < PAIRS:
                 load_pair(s // PAIR + 2)
             if_tile(leave_psum, s - 4)
-            if_tile(minus_row_sum, s - 1)
+            if s <= LEAD_FROM + 1:
+                if_tile(minus_row_sum, s - 1)
+            if s > LEAD_FROM:
+                if_tile(minus_row_sum, s)
             if_tile(scale_dk, s - 3, 0)
             if_tile(scale_dk, s - 3, 1)
             if_tile(turn_dl, s - 2, 0)
             if_tile(turn_dl, s - 2, 1)
             if_step(scale_rbf, s - 1, 0)
             if_step(scale_rbf, s - 1, 2)
-            if_tile(minus_sum_probs, s - 1)
+            if s <= LEAD_FROM + 1:
+                if_tile(minus_sum_probs, s - 1)
+            if s > LEAD_FROM:
+                if_tile(minus_sum_probs, s)
             if_tile(dot_with_x, s - 5)
             if_tile(quantise_and_multiply, s - 3)
             if_pair(x_reciprocal_lengths, s - 3)
@@ -373,7 +380,10 @@ def tile_rbf_softmax_layer_t_v_kernel(tc, x, kernel, rbf, probs, grad_out, out):
             if_tile(x_sum_of_squares, s - 1)
             if_pair(x_floor, s - 2)
             if_tile(project_and_store, s - 5)
-            if_tile(front, s)
+            if s <= LEAD_FROM:
+                if_tile(front, s)
+            if s >= LEAD_FROM:
+                if_tile(front, s + 1)
 
         open_pair(0)
         open_pair(1)

@@ -27,6 +27,7 @@ EPS = 1e-12
 LOGIT_SLOPE = 100.0 * 2.0 / 20.0
 
 LEAD_FROM = 4
+S_COLS = 704
 FLOPS = 2 * TOKENS * FEATURES * CLASSES
 
 
@@ -182,20 +183,19 @@ def tile_rbf_softmax_layer_t_v_kernel(tc, x, kernel, rbf, probs, grad_out, out):
 
         def minus_sum_probs(k):
             q, j = divmod(k, PAIR)
-            m_lo = work.tile([P, K_PASS], F32, tag="m_lo", bufs=4)
-            m_hi = work.tile([P, K_PASS], F32, tag="m_hi", bufs=4)
+            m_sb = work.tile([P, CLASSES], F32, tag="m", bufs=4)
             nc.gpsimd.tensor_scalar(
-                out=m_hi[:],
-                in0=inputs[q]["probs"][:, j, K_PASS:CLASSES],
+                out=m_sb[:, S_COLS:CLASSES],
+                in0=inputs[q]["probs"][:, j, S_COLS:CLASSES],
                 scalar1=row_sum_of[k][:],
                 scalar2=-1.0,
                 op0=ALU.mult,
                 op1=ALU.mult,
             )
             nc.scalar.activation(
-                out=m_lo[:], in_=inputs[q]["probs"][:, j, 0:K_PASS], func=ACT.Copy, scale=minus_sum_of[k][:]
+                out=m_sb[:, 0:S_COLS], in_=inputs[q]["probs"][:, j, 0:S_COLS], func=ACT.Copy, scale=minus_sum_of[k][:]
             )
-            m_of[k] = [m_lo, m_hi]
+            m_of[k] = m_sb
 
         def minus_row_sum(k):
             minus_sum = small.tile([P, 1], F32, tag="minus_sum")
@@ -260,7 +260,7 @@ def tile_rbf_softmax_layer_t_v_kernel(tc, x, kernel, rbf, probs, grad_out, out):
                 )
                 nc.tensor.matmul(
                     out=dl_turned[:, t, :],
-                    lhsT=m_of[k][g][:, t * P : (t + 1) * P],
+                    lhsT=m_of[k][:, c0 : c0 + P],
                     rhs=ident_f32[:],
                     is_transpose=True,
                     start=False,
@@ -438,8 +438,10 @@ def tile_rbf_softmax_layer_t_v_kernel(tc, x, kernel, rbf, probs, grad_out, out):
         turn_rbf(1, 0, 2)
         x_sum_of_squares(1)
         x_floor(0)
+        open_pair(3)
+        load_front(3, 0, PAIR)
         load_x(2)
-        load_pair(3)
+        load_rbf(3)
         front(2)
         for s in range(3, TILES + 5):
             step(s)

@@ -50,8 +50,8 @@ def tile_rbf_softmax_layer_t_v_kernel(tc, x, kernel, rbf, probs, grad_out, out):
         loads = stack.enter_context(tc.tile_pool(name="loads", bufs=3))
         work = stack.enter_context(tc.tile_pool(name="work", bufs=3))
         small = stack.enter_context(tc.tile_pool(name="small", bufs=8))
-        psum_dl = stack.enter_context(tc.psum_pool(name="psum_dl", bufs=2))
-        psum_rbf = stack.enter_context(tc.psum_pool(name="psum_rbf", bufs=4))
+        psum_dl = stack.enter_context(tc.psum_pool(name="psum_dl", bufs=3))
+        psum_rbf = stack.enter_context(tc.psum_pool(name="psum_rbf", bufs=3))
         psum_de = stack.enter_context(tc.psum_pool(name="psum_de", bufs=2))
         stack.enter_context(tc.manual_schedule())
 
@@ -302,7 +302,7 @@ def tile_rbf_softmax_layer_t_v_kernel(tc, x, kernel, rbf, probs, grad_out, out):
 
         def leave_psum(k):
             q, j = divmod(k, PAIR)
-            out_sb = work.tile([P, FEATURES], F32, tag="out", bufs=4)
+            out_sb = work.tile([P, FEATURES], F32, tag="out", bufs=6)
             for n in range(N_HALVES):
                 nc.scalar.activation(
                     out=out_sb[:, n * N_COLS : (n + 1) * N_COLS], in_=de_of[k][n][:], func=ACT.Copy, scale=rx_of[q][:, j : j + 1]

@@ -27,7 +27,7 @@ EPS = 1e-12
 LOGIT_SLOPE = 100.0 * 2.0 / 20.0
 
 LEAD_FROM = 4
-S_COLS = 704
+S_COLS = 640
 FLOPS = 2 * TOKENS * FEATURES * CLASSES
 
 
@@ -74,8 +74,10 @@ def tile_rbf_softmax_layer_t_v_kernel(tc, x, kernel, rbf, probs, grad_out, out):
         k_codes = keep.tile([P, PASSES, FEATURES], U32, align_bytes=64)
         k_scales = keep.tile([P, PASSES, FEATURES], U8, align_bytes=64)
         k_squares = keep.tile([P, PASSES, PACK], F32)
-        gram_banks = [psum_de.tile([P, PACK, P], F32, tag="de", name="gram%d" % n) for n in range(2)]
-        gram_banks += [psum_dl.tile([P, PACK, P], F32, tag="dl_turned", name="gram%d" % n) for n in range(2, 4)]
+        gram_of = {}
+        for t in range(PACK):
+            pool, tag = (psum_de, "de") if t < 2 else (psum_dl, "dl_turned")
+            gram_of[0, t] = pool.tile([P, P], F32, tag=tag, name="gram0%d" % t)
         rk10 = keep.tile([P, PASSES, PACK], F32)
         k_floor = keep.tile([P, PASSES, PACK], F32)
 
@@ -102,7 +104,7 @@ def tile_rbf_softmax_layer_t_v_kernel(tc, x, kernel, rbf, probs, grad_out, out):
             c0 = g * K_PASS + t * P
             block = k_rows[:, i, c0 : c0 + P]
             nc.tensor.matmul(
-                out=gram_banks[t][:, g, :], lhsT=block, rhs=block, start=(i == 0), stop=(i == D_TILES - 1)
+                out=gram_of[g, t][:], lhsT=block, rhs=block, start=(i == 0), stop=(i == D_TILES - 1)
             )
 
         def gram_diagonals(g):
@@ -110,7 +112,7 @@ def tile_rbf_softmax_layer_t_v_kernel(tc, x, kernel, rbf, probs, grad_out, out):
                 diagonal = work.tile([P, P], BF16, tag="unread_d")
                 nc.vector.scalar_tensor_tensor(
                     out=diagonal[:],
-                    in0=gram_banks[t][:, g, :],
+                    in0=gram_of[g, t][:],
                     scalar=1.0,
                     in1=ident_f32[:],
                     op0=ALU.mult,
@@ -406,20 +408,22 @@ def tile_rbf_softmax_layer_t_v_kernel(tc, x, kernel, rbf, probs, grad_out, out):
             if i == 5:
                 front(0)
         for t in range(PACK):
+            pool, tag = (psum_dl, "dl_turned") if t == 0 else (psum_rbf, "rbf_turned")
+            gram_of[1, t] = pool.tile([P, P], F32, tag=tag, name="gram1%d" % t)
             for i in range(D_TILES):
                 gram(1, t, i)
         turn_rbf(0, 0, 0)
         turn_rbf(0, 0, 2)
         turn_rbf(0, 1, 0)
         turn_rbf(0, 1, 2)
-        front(1)
         minus_row_sum(0)
         minus_sum_probs(0)
+        gram_diagonals(0)
+        front(1)
         minus_row_sum(1)
         minus_sum_probs(1)
         load_x(1)
         load_pair(2)
-        gram_diagonals(0)
         gram_diagonals(1)
         kernel_floor()
         kernel_reciprocal_lengths()

from contextlib import ExitStack

import concourse.mybir as mybir
from concourse.masks import make_identity

F32 = mybir.dt.float32
BF16 = mybir.dt.bfloat16
U32 = mybir.dt.uint32
U8 = mybir.dt.uint8
E4M3X4 = mybir.dt.float8_e4m3fn_x4
E5M2X4 = mybir.dt.float8_e5m2_x4
ACT = mybir.ActivationFunctionType
ALU = mybir.AluOpType

TOKENS, FEATURES, CLASSES = 2048, 1024, 1024
P = 128
PACK = 4
K_PASS = P * PACK
PASSES = CLASSES // K_PASS
N_COLS = 512
N_HALVES = FEATURES // N_COLS
PAIR = 2
PAIRS = TOKENS // (PAIR * P)
TILES = TOKENS // P
D_TILES = FEATURES // P
EPS = 1e-12
LOGIT_SLOPE = 100.0 * 2.0 / 20.0

LEAD_FROM = 4
S_COLS = 640
FLOPS = 2 * TOKENS * FEATURES * CLASSES


def tile_rbf_softmax_layer_t_v_kernel(tc, x, kernel, rbf, probs, grad_out, out):
    nc = tc.nc

    def by_pairs(dram):
        return dram.rearrange("(q p j) c -> q p j c", p=P, j=PAIR)

    x_pairs, rbf_pairs, probs_pairs, grad_pairs, out_pairs = (
        by_pairs(x),
        by_pairs(rbf),
        by_pairs(probs),
        by_pairs(grad_out),
        by_pairs(out),
    )

    with ExitStack() as stack:
        keep = stack.enter_context(tc.tile_pool(name="keep", bufs=1))
        loads = stack.enter_context(tc.tile_pool(name="loads", bufs=3))
        work = stack.enter_context(tc.tile_pool(name="work", bufs=3))
        small = stack.enter_context(tc.tile_pool(name="small", bufs=8))
        psum_dl = stack.enter_context(tc.psum_pool(name="psum_dl", bufs=3))
        psum_rbf = stack.enter_context(tc.psum_pool(name="psum_rbf", bufs=3))
        psum_de = stack.enter_context(tc.psum_pool(name="psum_de", bufs=2))
        stack.enter_context(tc.manual_schedule())

        ident_f32 = keep.tile([P, P], F32)
        make_identity(nc, ident_f32[:])
        ident_bf16 = keep.tile([P, P], BF16)
        make_identity(nc, ident_bf16[:])
        one = keep.tile([P, 1], F32)
        nc.vector.memset(one[:], 1.0)
        minus_eps = keep.tile([P, 1], F32)
        nc.vector.memset(minus_eps[:], -EPS)
        warm = keep.tile([P, 1], F32)
        nc.scalar.activation(out=warm[:], in_=one[:], func=ACT.Sqrt)

        zeros = keep.tile([P, P], F32)
        nc.vector.memset(zeros[:], 0.0)

        k_rows = keep.tile([P, D_TILES, CLASSES], BF16)
        k_grouped = keep.tile([P, PASSES, FEATURES, PACK], BF16, align_bytes=64)
        k_codes = keep.tile([P, PASSES, FEATURES], U32, align_bytes=64)
        k_scales = keep.tile([P, PASSES, FEATURES], U8, align_bytes=64)
        k_squares = keep.tile([P, PASSES, PACK], F32)
        gram_of = {}
        for t in range(PACK):
            pool, tag = (psum_de, "de") if t < 2 else (psum_dl, "dl_turned")
            gram_of[0, t] = pool.tile([P, P], F32, tag=tag, name="gram0%d" % t)
        rk10 = keep.tile([P, PASSES, PACK], F32)
        k_floor = keep.tile([P, PASSES, PACK], F32)

        def load_kernel(i, tiles):
            nc.sync.dma_start(
                out=k_rows[:, i : i + tiles, :],
                in_=kernel[i * P : (i + tiles) * P, :].rearrange("(i p) c -> p i c", p=P),
            )

        def turn_kernel(i):
            k_turned = psum_rbf.tile([P, PASSES, PACK, P], BF16, tag="rbf_turned")
            for g in range(PASSES):
                for t in range(PACK):
                    c0 = g * K_PASS + t * P
                    nc.tensor.transpose(k_turned[:, g, t, :], k_rows[:, i, c0 : c0 + P], ident_bf16[:])
            grouped_view = k_grouped[:, :, i * P : (i + 1) * P, :]
            turned_view = k_turned[:].rearrange("p g t r -> p g r t")
            if i in (0, 2, 4):
                nc.vector.tensor_copy(out=grouped_view, in_=turned_view)
            else:
                nc.scalar.copy(out=grouped_view, in_=turned_view)

        def gram(g, t, i):
            c0 = g * K_PASS + t * P
            block = k_rows[:, i, c0 : c0 + P]
            nc.tensor.matmul(
                out=gram_of[g, t][:], lhsT=block, rhs=block, start=(i == 0), stop=(i == D_TILES - 1)
            )

        def gram_diagonals(g):
            for t in range(PACK):
                diagonal = work.tile([P, P], BF16, tag="unread_d")
                nc.vector.scalar_tensor_tensor(
                    out=diagonal[:],
                    in0=gram_of[g, t][:],
                    scalar=1.0,
                    in1=ident_f32[:],
                    op0=ALU.mult,
                    op1=ALU.mult,
                    accum_out=k_squares[:, g, t : t + 1],
                )

        def kernel_floor():
            nc.vector.tensor_scalar_max(out=k_floor[:], in0=k_squares[:], scalar1=EPS)

        def kernel_reciprocal_lengths():
            inv = keep.tile([P, PASSES, PACK], F32)
            nc.vector.reciprocal(out=inv[:], in_=k_floor[:])
            nc.scalar.activation(out=rk10[:], in_=inv[:], func=ACT.Sqrt, scale=LOGIT_SLOPE * LOGIT_SLOPE)

        def quantise_kernel(g):
            nc.vector.quantize_mx(
                out=k_codes[:, g, :].bitcast(E4M3X4),
                scales=k_scales[:, g, :],
                in_=k_grouped[:, g, :, :].rearrange("p d t -> p (d t)"),
            )

        def warm_up(passes):
            bank = psum_rbf.tile([P, P], F32, tag="rbf_turned", name="warm_bank")
            for n in range(passes):
                nc.tensor.matmul(out=bank[:], lhsT=zeros[:], rhs=zeros[:], start=True, stop=True)

        inputs, t_of, m_of, r_of, dl_of, dk_of, de_of, out_of = {}, {}, {}, {}, {}, {}, {}, {}
        xx_of, xx_floor_of, inv_xx_of, rx_of, pull_of, minus_sum_of = {}, {}, {}, {}, {}, {}
        x_of, row_sum_of, rbf_turned_of = {}, {}, {}

        def open_pair(q):
            inputs[q] = {
                "probs": loads.tile([P, PAIR, CLASSES], F32, tag="probs", name="probs"),
                "grad": loads.tile([P, PAIR, CLASSES], BF16, tag="grad", name="grad"),
                "rbf": loads.tile([P, PAIR, CLASSES], F32, tag="rbf", name="rbf"),
            }

        def load_front(q, j, tiles):
            nc.sync.dma_start(out=inputs[q]["probs"][:, j : j + tiles, :], in_=probs_pairs[q][:, j : j + tiles, :])
            nc.sync.dma_start(out=inputs[q]["grad"][:, j : j + tiles, :], in_=grad_pairs[q][:, j : j + tiles, :])

        def load_rbf(q):
            nc.sync.dma_start(out=inputs[q]["rbf"][:], in_=rbf_pairs[q])

        def load_pair(q):
            open_pair(q)
            load_front(q, 0, PAIR)
            load_rbf(q)

        def load_x(q):
            x_sb = loads.tile([P, PAIR, FEATURES], BF16, tag="x", bufs=5)
            nc.sync.dma_start(out=x_sb[:], in_=x_pairs[q])
            x_of[q] = x_sb

        def front(k):
            q, j = divmod(k, PAIR)
            t_sb = work.tile([P, CLASSES], F32, tag="t", bufs=5)
            row_sum = small.tile([P, 1], F32, tag="row_sum")
            nc.vector.scalar_tensor_tensor(
                out=t_sb[:],
                in0=inputs[q]["grad"][:, j, :],
                scalar=1.0,
                in1=inputs[q]["probs"][:, j, :],
                op0=ALU.mult,
                op1=ALU.mult,
                accum_out=row_sum[:],
            )
            t_of[k], row_sum_of[k] = t_sb, row_sum

        def minus_sum_probs(k):
            q, j = divmod(k, PAIR)
            m_sb = work.tile([P, CLASSES], F32, tag="m", bufs=4)
            nc.gpsimd.tensor_scalar(
                out=m_sb[:, S_COLS:CLASSES],
                in0=inputs[q]["probs"][:, j, S_COLS:CLASSES],
                scalar1=row_sum_of[k][:],
                scalar2=-1.0,
                op0=ALU.mult,
                op1=ALU.mult,
            )
            nc.scalar.activation(
                out=m_sb[:, 0:S_COLS], in_=inputs[q]["probs"][:, j, 0:S_COLS], func=ACT.Copy, scale=minus_sum_of[k][:]
            )
            m_of[k] = m_sb

        def minus_row_sum(k):
            minus_sum = small.tile([P, 1], F32, tag="minus_sum")
            nc.scalar.mul(out=minus_sum[:], in_=row_sum_of[k][:], mul=-1.0)
            minus_sum_of[k] = minus_sum

        def x_sum_of_squares(k):
            q, j = divmod(k, PAIR)
            if j == 0:
                xx_of[q] = small.tile([P, PAIR], F32, tag="xx", name="xx")
            squares = work.tile([P, FEATURES], BF16, tag="unread_s")
            nc.scalar.activation(
                out=squares[:], in_=x_of[q][:, j, :], func=ACT.Square, accum_out=xx_of[q][:, j : j + 1]
            )

        def x_floor(q):
            xx_floor = small.tile([P, PAIR], F32, tag="xx_floor")
            above = small.tile([P, PAIR], F32, tag="above")
            nc.scalar.activation(out=above[:], in_=xx_of[q][:], func=ACT.Relu, bias=minus_eps[:])
            nc.scalar.activation(out=xx_floor[:], in_=above[:], func=ACT.Identity, scale=-1.0, bias=minus_eps[:])
            xx_floor_of[q] = xx_floor

        def x_reciprocal_lengths(q):
            inv_xx = small.tile([P, PAIR], F32, tag="inv_xx")
            nc.vector.reciprocal(out=inv_xx[:], in_=xx_floor_of[q][:])
            rx = small.tile([P, PAIR], F32, tag="rx")
            nc.scalar.activation(out=rx[:], in_=inv_xx[:], func=ACT.Sqrt, scale=-1.0)
            inv_xx_of[q], rx_of[q] = inv_xx, rx

        def turn_rbf(q, g, t0):
            rbf_turned = psum_rbf.tile([P, 2, PAIR * P], F32, tag="rbf_turned")
            for h in range(2):
                c0 = g * K_PASS + (t0 + h) * P
                for j in range(PAIR):
                    nc.tensor.transpose(
                        rbf_turned[:, h, j * P : (j + 1) * P], inputs[q]["rbf"][:, j, c0 : c0 + P], ident_f32[:]
                    )
            rbf_turned_of[q, g, t0] = rbf_turned

        def scale_rbf(q, g, t0):
            if (g, t0) == (0, 0):
                r_of[q] = work.tile([P, PASSES, PACK, PAIR * P], F32, tag="r", bufs=2, name="r")
            for h in range(2):
                nc.scalar.activation(
                    out=r_of[q][:, g, t0 + h, :],
                    in_=rbf_turned_of[q, g, t0][:, h, :],
                    func=ACT.Copy,
                    scale=rk10[:, g, t0 + h : t0 + h + 1],
                )

        def turn_dl(k, g):
            dl_turned = psum_dl.tile([P, PACK, P], F32, tag="dl_turned")
            for t in range(PACK):
                c0 = g * K_PASS + t * P
                nc.tensor.matmul(
                    out=dl_turned[:, t, :],
                    lhsT=t_of[k][:, c0 : c0 + P],
                    rhs=ident_f32[:],
                    is_transpose=True,
                    start=True,
                    stop=False,
                )
                nc.tensor.matmul(
                    out=dl_turned[:, t, :],
                    lhsT=m_of[k][:, c0 : c0 + P],
                    rhs=ident_f32[:],
                    is_transpose=True,
                    start=False,
                    stop=True,
                )
            dl_of[k, g] = dl_turned

        def scale_dk(k, g):
            q, j = divmod(k, PAIR)
            if g == 0:
                dk_of[k] = work.tile([P, PASSES, P, PACK], BF16, tag="dk_grouped", align_bytes=64, name="dk_grouped")
            nc.vector.tensor_tensor(
                out=dk_of[k][:, g, :, :].rearrange("p (c i) t -> p c t i", i=8),
                in0=dl_of[k, g][:].rearrange("p t (c i) -> p c t i", i=8),
                in1=r_of[q][:, g, :, j * P : (j + 1) * P].rearrange("p t (c i) -> p c t i", i=8),
                op=ALU.mult,
            )

        def quantise_and_multiply(k):
            dk_codes = work.tile([P, PASSES * P], U32, tag="dk_codes", align_bytes=64)
            dk_scales = work.tile([P, PASSES * P], U8, tag="dk_scales", align_bytes=64)
            nc.vector.quantize_mx(
                out=dk_codes[:].bitcast(E5M2X4),
                scales=dk_scales[:],
                in_=dk_of[k][:].rearrange("p g b t -> p (g b t)"),
            )
            de_of[k] = [psum_de.tile([P, N_COLS], F32, tag="de", name="de%d" % n) for n in range(N_HALVES)]
            for g in range(PASSES):
                for n in range(N_HALVES):
                    nc.tensor.matmul_mx(
                        out=de_of[k][n][:],
                        lhsT=dk_codes[:, g * P : (g + 1) * P].bitcast(E5M2X4),
                        lhsT_scale=dk_scales[:, g * P : (g + 1) * P],
                        rhs=k_codes[:, g, n * N_COLS : (n + 1) * N_COLS].bitcast(E4M3X4),
                        rhs_scale=k_scales[:, g, n * N_COLS : (n + 1) * N_COLS],
                        start=(g == 0),
                        stop=(g == PASSES - 1),
                    )

        def leave_psum(k):
            q, j = divmod(k, PAIR)
            out_sb = work.tile([P, FEATURES], F32, tag="out", bufs=6)
            for n in range(N_HALVES):
                nc.scalar.activation(
                    out=out_sb[:, n * N_COLS : (n + 1) * N_COLS], in_=de_of[k][n][:], func=ACT.Copy, scale=rx_of[q][:, j : j + 1]
                )
            out_of[k] = out_sb

        def dot_with_x(k):
            q, j = divmod(k, PAIR)
            products = work.tile([P, FEATURES], BF16, tag="unread_v")
            pull = small.tile([P, 1], F32, tag="pull")
            nc.vector.scalar_tensor_tensor(
                out=products[:],
                in0=out_of[k][:],
                scalar=inv_xx_of[q][:, j : j + 1],
                in1=x_of[q][:, j, :],
                op0=ALU.mult,
                op1=ALU.mult,
                accum_out=pull[:],
            )
            pull_of[k] = pull

        def project_and_store(k):
            q, j = divmod(k, PAIR)
            pieces = N_HALVES if k == TILES - 1 else 1
            width = FEATURES // pieces
            for n in range(pieces):
                cols = slice(n * width, (n + 1) * width)
                nc.vector.scalar_tensor_tensor(
                    out=out_of[k][:, cols],
                    in0=x_of[q][:, j, cols],
                    scalar=pull_of[k][:],
                    in1=out_of[k][:, cols],
                    op0=ALU.mult,
                    op1=ALU.add,
                )
                nc.sync.dma_start(out=out_pairs[q][:, j, cols], in_=out_of[k][:, cols])

        def if_tile(stage, k, *more):
            if 0 <= k < TILES:
                stage(k, *more)

        def if_pair(stage, k):
            if k % PAIR == 0 and 0 <= k < TILES:
                stage(k // PAIR)

        def if_step(stage, s, t0):
            if 0 <= s < TILES:
                stage(s // PAIR, s % PAIR, t0)

        def step(s):
            if s % PAIR == 0 and s // PAIR + 1 < PAIRS:
                load_x(s // PAIR + 1)
            if s % PAIR == 0 and s // PAIR + 2 < PAIRS:
                load_pair(s // PAIR + 2)
            if_tile(leave_psum, s - 4)
            if s <= LEAD_FROM + 1:
                if_tile(minus_row_sum, s - 1)
            if s > LEAD_FROM:
                if_tile(minus_row_sum, s)
            if_tile(scale_dk, s - 3, 0)
            if_tile(scale_dk, s - 3, 1)
            if_tile(turn_dl, s - 2, 0)
            if_tile(turn_dl, s - 2, 1)
            if_step(scale_rbf, s - 1, 0)
            if_step(scale_rbf, s - 1, 2)
            if s <= LEAD_FROM + 1:
                if_tile(minus_sum_probs, s - 1)
            if s > LEAD_FROM:
                if_tile(minus_sum_probs, s)
            if_tile(dot_with_x, s - 5)
            if_tile(quantise_and_multiply, s - 3)
            if_pair(x_reciprocal_lengths, s - 3)
            if_step(turn_rbf, s, 0)
            if_step(turn_rbf, s, 2)
            if_tile(x_sum_of_squares, s - 1)
            if_pair(x_floor, s - 2)
            if_tile(project_and_store, s - 5)
            if s <= LEAD_FROM:
                if_tile(front, s)
            if s >= LEAD_FROM:
                if_tile(front, s + 1)

        open_pair(0)
        open_pair(1)
        load_kernel(0, 1)
        load_kernel(1, 1)
        load_kernel(2, 2)
        load_kernel(4, 2)
        load_front(0, 0, 1)
        load_kernel(6, 2)
        load_front(0, 1, 1)
        load_rbf(0)
        load_x(0)
        load_front(1, 0, 2)
        load_rbf(1)
        warm_up(6)
        for i in range(D_TILES):
            turn_kernel(i)
            for t in range(PACK):
                gram(0, t, i)
            if i == 5:
                front(0)
        for t in range(PACK):
            pool, tag = (psum_dl, "dl_turned") if t == 0 else (psum_rbf, "rbf_turned")
            gram_of[1, t] = pool.tile([P, P], F32, tag=tag, name="gram1%d" % t)
            for i in range(D_TILES):
                gram(1, t, i)
        turn_rbf(0, 0, 0)
        turn_rbf(0, 0, 2)
        turn_rbf(0, 1, 0)
        turn_rbf(0, 1, 2)
        minus_row_sum(0)
        minus_sum_probs(0)
        gram_diagonals(0)
        front(1)
        minus_row_sum(1)
        minus_sum_probs(1)
        load_x(1)
        load_pair(2)
        gram_diagonals(1)
        kernel_floor()
        kernel_reciprocal_lengths()
        warm_up(3)
        turn_dl(0, 0)
        turn_dl(0, 1)
        scale_rbf(0, 0, 0)
        scale_rbf(0, 0, 2)
        scale_rbf(0, 1, 0)
        scale_rbf(0, 1, 2)
        x_sum_of_squares(0)
        quantise_kernel(0)
        quantise_kernel(1)
        warm_up(6)
        turn_rbf(1, 0, 0)
        turn_rbf(1, 0, 2)
        x_sum_of_squares(1)
        x_floor(0)
        open_pair(3)
        load_front(3, 0, PAIR)
        load_x(2)
        load_rbf(3)
        front(2)
        for s in range(3, TILES + 5):
            step(s)
